import numpy as np
import ml_dtypes

BF16 = ml_dtypes.bfloat16


def bf(x):
    return np.asarray(x, np.float32).astype(BF16)


def f32(x):
    return np.asarray(x, np.float32)


def f64(x):
    return np.asarray(x).astype(np.float64)


def striped(idx):
    return np.tile(idx.reshape(-1, 16).T, (8, 1))


C, V, P, N, S = 512, 2048, 128, 1024, 2048
TAU, TAU_EPS, BN_EPS, Q, GAIN = 0.1, 1e-8, 1e-5, 0.015625, 0.08


def setup_inputs():
    vertex_feat = bf(np.random.standard_normal((C, V)))
    member = np.random.random((V, N)) < Q
    incidence = bf(member * (0.1 + 0.1 * np.random.random((V, N))))
    inv_deg = f32(0.75 + 0.5 * np.random.random((1, N)))
    proj_w = bf(np.random.standard_normal((C, P)) / np.sqrt(C))
    bn_gamma = f32(GAIN * (0.5 + np.random.random((P, 1))))
    bn_beta = f32(0.01 * np.random.standard_normal((P, 1)))
    bn_mean = f32(0.1 * np.random.standard_normal((P, 1)))
    bn_var = f32(0.5 + np.random.random((P, 1)))
    base = f32(np.random.standard_normal((C, S)))
    return {"vertex_feat": vertex_feat, "incidence": incidence, "inv_deg": inv_deg, "proj_w": proj_w, "bn_gamma": bn_gamma, "bn_beta": bn_beta, "bn_mean": bn_mean, "bn_var": bn_var, "base": base, "offs": striped(np.random.permutation(S)[:N])}


def reference(vertex_feat, incidence, inv_deg, proj_w, bn_gamma, bn_beta, bn_mean, bn_var, base, offs):
    idx = offs[:16].T.reshape(-1)
    v = f64(vertex_feat)
    d = f64(inv_deg)
    k = (f64(proj_w).T @ v - f64(bn_mean)) * (f64(bn_gamma) / np.sqrt(f64(bn_var) + BN_EPS)) + f64(bn_beta)
    proto = (k @ f64(incidence)) * d
    z = (2.0 * (k.T @ proto) - np.sum(k * k, axis=0)[:, None]) / (TAU + TAU_EPS)
    e = np.exp(z - np.max(z, axis=0, keepdims=True))
    a = e / np.sum(e, axis=0, keepdims=True)
    out = f64(base).copy()
    out[:, idx] = (v @ a) * d
    return out

@@ -1,0 +1,208 @@
+import concourse.mybir as mybir
+from concourse.masks import make_identity
+
+C, V, P, N, S = 512, 2048, 128, 1024, 2048
+TEMPERATURE = 0.1 + 1e-8
+BN_EPS = 1e-5
+FLOPS = 2 * (C * P * V + 2 * P * V * N + C * V * N)
+
+BF16, F32, U16 = mybir.dt.bfloat16, mybir.dt.float32, mybir.dt.uint16
+ALU = mybir.AluOpType
+ACT = mybir.ActivationFunctionType
+AXIS = mybir.AxisListType
+
+LANES = 128
+BANK = 512
+CB = C // LANES
+NB = V // LANES
+JC = N // BANK
+QUARTERS = BANK // LANES
+
+
+def block(i):
+    return slice(i * LANES, (i + 1) * LANES)
+
+
+def chunk(i):
+    return slice(i * BANK, (i + 1) * BANK)
+
+
+def tile_whnnaggregator_b_kernel(
+    tc, vertex_feat, incidence, inv_deg, proj_w, bn_gamma, bn_beta, bn_mean, bn_var, base, offs, out
+):
+    nc = tc.nc
+    with (
+        tc.tile_pool(name="held", bufs=1) as held,
+        tc.tile_pool(name="ring", bufs=2) as ring,
+        tc.psum_pool(name="psum_work", bufs=3) as psum_work,
+        tc.psum_pool(name="psum_long", bufs=3) as psum_long,
+        tc.psum_pool(name="psum_small", bufs=1) as psum_small,
+    ):
+        queues = (nc.sync, nc.scalar)
+
+        offsets = held.tile([LANES, N // 16], U16, name="offsets")
+        nc.sync.dma_start(offsets[:], offs)
+
+        weights = held.tile([LANES, CB, P], BF16, name="weights")
+        nc.sync.dma_start(weights[:], proj_w.rearrange("(cb c) p -> c cb p", c=LANES))
+
+        bn_rows = held.tile([LANES, LANES], F32, name="bn_rows")
+        nc.vector.memset(bn_rows[:], 0.0)
+        for row, vector in enumerate((bn_gamma, bn_beta, bn_mean, bn_var)):
+            nc.scalar.dma_start(bn_rows[row : row + 1, :], vector.rearrange("p one -> one p"))
+
+        feat = [held.tile([LANES, V], BF16, name=f"feat{cb}") for cb in range(CB)]
+        for cb in range(CB):
+            queues[cb % 2].dma_start(feat[cb][:], vertex_feat[block(cb), :])
+
+        deg = held.tile([LANES, N], F32, name="deg")
+        nc.scalar.dma_start(deg[:], inv_deg[0, :].partition_broadcast(LANES))
+
+        member = held.tile([LANES, NB, N], BF16, name="member")
+        incidence_blocks = incidence.rearrange("(nb n) j -> n nb j", n=LANES)
+        for g in range(NB // 4):
+            queues[g % 2].dma_start(member[:, 4 * g : 4 * g + 4, :], incidence_blocks[:, 4 * g : 4 * g + 4, :])
+
+        window = [held.tile([LANES, S], F32, name=f"window{cb}") for cb in range(CB)]
+        for cb in range(CB):
+            queues[cb % 2].dma_start(window[cb][:], base[block(cb), :])
+
+        ident_f = held.tile([LANES, LANES], F32, name="ident_f")
+        make_identity(nc, ident_f[:])
+        ident_b = held.tile([LANES, LANES], BF16, name="ident_b")
+        nc.vector.tensor_copy(ident_b[:], ident_f[:])
+        ones_b = held.tile([LANES, LANES], BF16, name="ones_b")
+        nc.vector.memset(ones_b[:], 1.0)
+        ones_f = held.tile([LANES, LANES], F32, name="ones_f")
+        nc.vector.memset(ones_f[:], 1.0)
+
+        bn_ps = psum_work.tile([LANES, LANES], F32, name="bn_ps", tag="work")
+        nc.tensor.transpose(bn_ps[:], bn_rows[:], ident_f[:])
+        bn = held.tile([LANES, 4], F32, name="bn")
+        nc.vector.tensor_copy(bn[:], bn_ps[:, 0:4])
+        k_scale = held.tile([LANES, 1], F32, name="k_scale")
+        k_shift = held.tile([LANES, 1], F32, name="k_shift")
+        nc.vector.tensor_scalar_add(k_scale[:], bn[:, 3:4], BN_EPS)
+        nc.scalar.sqrt(k_scale[:], k_scale[:])
+        nc.vector.reciprocal(k_scale[:], k_scale[:])
+        nc.vector.tensor_mul(k_scale[:], k_scale[:], bn[:, 0:1])
+        nc.vector.tensor_mul(k_shift[:], bn[:, 2:3], k_scale[:])
+        nc.vector.tensor_sub(k_shift[:], bn[:, 1:2], k_shift[:])
+
+        keys = held.tile([LANES, V], BF16, name="keys")
+        for i in range(V // BANK):
+            k_ps = psum_work.tile([LANES, BANK], F32, name="k_ps", tag="work")
+            for cb in range(CB):
+                nc.tensor.matmul(k_ps[:], weights[:, cb, :], feat[cb][:, chunk(i)], start=(cb == 0), stop=(cb == CB - 1))
+            nc.scalar.activation(keys[:, chunk(i)], k_ps[:], ACT.Identity, bias=k_shift[:], scale=k_scale[:])
+
+        keys_t = held.tile([LANES, NB, P], BF16, name="keys_t")
+        for g in range(NB // 4):
+            kt_ps = psum_work.tile([LANES, 4, P], BF16, name="kt_ps", tag="work")
+            for i in range(4):
+                nc.tensor.transpose(kt_ps[:, i, :], keys[:, block(4 * g + i)], ident_b[:])
+            nc.vector.tensor_copy(keys_t[:, 4 * g : 4 * g + 4, :], kt_ps[:])
+
+        squares = held.tile([LANES, NB, P], F32, name="squares")
+        nc.scalar.square(squares[:], keys_t[:])
+        norm = held.tile([LANES, NB], F32, name="norm")
+        nc.vector.reduce_sum(norm[:], squares[:], axis=AXIS.X)
+        neg_half_norm = held.tile([LANES, NB], F32, name="neg_half_norm")
+        nc.vector.tensor_scalar_mul(neg_half_norm[:], norm[:], -0.5)
+        exp_bias = held.tile([LANES, NB], F32, name="exp_bias")
+        nc.vector.tensor_scalar_mul(exp_bias[:], norm[:], -1.0 / TEMPERATURE)
+
+        feat_t = held.tile([LANES, NB, CB, LANES], BF16, name="feat_t")
+        for nb in range(NB):
+            ft_ps = psum_work.tile([LANES, CB, LANES], BF16, name="ft_ps", tag="work")
+            for cb in range(CB):
+                nc.tensor.transpose(ft_ps[:, cb, :], feat[cb][:, block(nb)], ident_b[:])
+            if nb % 2 == 0:
+                nc.scalar.copy(feat_t[:, nb, :, :], ft_ps[:])
+            else:
+                nc.vector.tensor_copy(feat_t[:, nb, :, :], ft_ps[:])
+
+        proto = held.tile([LANES, N], BF16, name="proto")
+        proto_ps = [psum_long.tile([LANES, BANK], F32, name=f"proto_ps{jc}", tag="long") for jc in range(JC)]
+        for nb in range(NB):
+            for jc in range(JC):
+                nc.tensor.matmul(
+                    proto_ps[jc][:], keys_t[:, nb, :], member[:, nb, chunk(jc)], start=(nb == 0), stop=(nb == NB - 1)
+                )
+        for jc in range(JC):
+            nc.vector.tensor_tensor(proto[:, chunk(jc)], proto_ps[jc][:], deg[:, chunk(jc)], ALU.mult)
+
+        lane_max = [held.tile([LANES, BANK], F32, name=f"lane_max{jc}") for jc in range(JC)]
+        shift = [held.tile([LANES, BANK], BF16, name=f"shift{jc}") for jc in range(JC)]
+        soft = [held.tile([LANES, NB, BANK], BF16, name=f"soft{jc}") for jc in range(JC)]
+
+        def inner_products(jc, nb, closed):
+            z_ps = psum_work.tile([LANES, BANK], F32, name="z_ps", tag="work")
+            nc.tensor.matmul(z_ps[:], keys[:, block(nb)], proto[:, chunk(jc)], start=True, stop=closed)
+            return z_ps
+
+        def first_pass(jc, nb):
+            z_ps = inner_products(jc, nb, True)
+            if nb == 0:
+                nc.vector.tensor_scalar_add(lane_max[jc][:], z_ps[:], neg_half_norm[:, 0:1])
+            else:
+                nc.vector.scalar_tensor_tensor(
+                    lane_max[jc][:], z_ps[:], neg_half_norm[:, nb : nb + 1], lane_max[jc][:], ALU.add, ALU.max
+                )
+
+        def maximum_over_lanes(jc):
+            lanes_ps = psum_work.tile([LANES, QUARTERS, LANES], F32, name="lanes_ps", tag="work")
+            for q in range(QUARTERS):
+                nc.tensor.transpose(lanes_ps[:, q, :], lane_max[jc][:, block(q)], ident_f[:])
+            neg_top = held.tile([LANES, QUARTERS], F32, name=f"neg_top{jc}")
+            nc.vector.tensor_reduce(neg_top[:], lanes_ps[:], axis=AXIS.X, op=ALU.max, negate=True)
+            for q in range(QUARTERS):
+                nc.vector.tensor_scalar_mul(shift[jc][:, block(q)], ident_f[:], neg_top[:, q : q + 1])
+
+        def second_pass(jc, nb):
+            z_ps = inner_products(jc, nb, False)
+            nc.tensor.matmul(z_ps[:], ones_b[:], shift[jc][:], start=False, stop=True)
+            nc.scalar.activation(
+                soft[jc][:, nb, :], z_ps[:], ACT.Exp, bias=exp_bias[:, nb : nb + 1], scale=2.0 / TEMPERATURE
+            )
+
+        def last_factor(jc):
+            sum_ps = psum_small.tile([LANES, QUARTERS], F32, name="sum_ps")
+            for q in range(QUARTERS):
+                for nb in range(NB):
+                    nc.tensor.matmul(
+                        sum_ps[:, q : q + 1], soft[jc][:, nb, block(q)], ones_b[:, 0:1], start=(nb == 0), stop=(nb == NB - 1)
+                    )
+            inv_sum = held.tile([LANES, QUARTERS], F32, name=f"inv_sum{jc}")
+            nc.vector.reciprocal(inv_sum[:], sum_ps[:])
+            diagonal = held.tile([LANES, BANK], F32, name=f"diagonal{jc}")
+            for q in range(QUARTERS):
+                nc.vector.tensor_scalar_mul(diagonal[:, block(q)], ident_f[:], inv_sum[:, q : q + 1])
+            spread_ps = psum_small.tile([LANES, BANK], F32, name="spread_ps")
+            nc.tensor.matmul(spread_ps[:], ones_f[:], diagonal[:], start=True, stop=True)
+            factor = held.tile([LANES, BANK], F32, name=f"factor{jc}")
+            nc.vector.tensor_tensor(factor[:], spread_ps[:], deg[:, chunk(jc)], ALU.mult)
+            return factor
+
+        for nb in range(NB):
+            first_pass(0, nb)
+        for jc in range(JC):
+            maximum_over_lanes(jc)
+            for nb in range(NB):
+                if jc + 1 < JC:
+                    first_pass(jc + 1, nb)
+                second_pass(jc, nb)
+            factor = last_factor(jc)
+
+            piece = offsets[:, jc * (BANK // 16) : (jc + 1) * (BANK // 16)]
+            for cb in range(CB):
+                agg_ps = psum_long.tile([LANES, BANK], F32, name="agg_ps", tag="long")
+                for nb in range(NB):
+                    nc.tensor.matmul(
+                        agg_ps[:], feat_t[:, nb, cb, :], soft[jc][:, nb, :], start=(nb == 0), stop=(nb == NB - 1)
+                    )
+                agg = ring.tile([LANES, BANK], F32, name="agg")
+                nc.scalar.copy(agg[:], agg_ps[:])
+                nc.vector.tensor_tensor(window[cb][:].indirect(piece), agg[:], factor[:], ALU.mult)
+                if jc == JC - 1:
+                    queues[cb % 2].dma_start(out[block(cb), :], window[cb][:])

@@ -1,3 +1,5 @@
+import math
+
 import concourse.mybir as mybir
 from concourse.masks import make_identity
 
@@ -17,6 +19,7 @@ CB = C // LANES
 NB = V // LANES
 JC = N // BANK
 QUARTERS = BANK // LANES
+GROUP = 4
 
 
 def block(i):
@@ -25,6 +28,10 @@ def block(i):
 
 def chunk(i):
     return slice(i * BANK, (i + 1) * BANK)
+
+
+def group(i):
+    return slice(i * GROUP, (i + 1) * GROUP)
 
 
 def tile_whnnaggregator_b_kernel(
@@ -40,33 +47,6 @@ def tile_whnnaggregator_b_kernel(
     ):
         queues = (nc.sync, nc.scalar)
 
-        offsets = held.tile([LANES, N // 16], U16, name="offsets")
-        nc.sync.dma_start(offsets[:], offs)
-
-        weights = held.tile([LANES, CB, P], BF16, name="weights")
-        nc.sync.dma_start(weights[:], proj_w.rearrange("(cb c) p -> c cb p", c=LANES))
-
-        bn_rows = held.tile([LANES, LANES], F32, name="bn_rows")
-        nc.vector.memset(bn_rows[:], 0.0)
-        for row, vector in enumerate((bn_gamma, bn_beta, bn_mean, bn_var)):
-            nc.scalar.dma_start(bn_rows[row : row + 1, :], vector.rearrange("p one -> one p"))
-
-        feat = [held.tile([LANES, V], BF16, name=f"feat{cb}") for cb in range(CB)]
-        for cb in range(CB):
-            queues[cb % 2].dma_start(feat[cb][:], vertex_feat[block(cb), :])
-
-        deg = held.tile([LANES, N], F32, name="deg")
-        nc.scalar.dma_start(deg[:], inv_deg[0, :].partition_broadcast(LANES))
-
-        member = held.tile([LANES, NB, N], BF16, name="member")
-        incidence_blocks = incidence.rearrange("(nb n) j -> n nb j", n=LANES)
-        for g in range(NB // 4):
-            queues[g % 2].dma_start(member[:, 4 * g : 4 * g + 4, :], incidence_blocks[:, 4 * g : 4 * g + 4, :])
-
-        window = [held.tile([LANES, S], F32, name=f"window{cb}") for cb in range(CB)]
-        for cb in range(CB):
-            queues[cb % 2].dma_start(window[cb][:], base[block(cb), :])
-
         ident_f = held.tile([LANES, LANES], F32, name="ident_f")
         make_identity(nc, ident_f[:])
         ident_b = held.tile([LANES, LANES], BF16, name="ident_b")
@@ -76,98 +56,57 @@ def tile_whnnaggregator_b_kernel(
         ones_f = held.tile([LANES, LANES], F32, name="ones_f")
         nc.vector.memset(ones_f[:], 1.0)
 
-        bn_ps = psum_work.tile([LANES, LANES], F32, name="bn_ps", tag="work")
-        nc.tensor.transpose(bn_ps[:], bn_rows[:], ident_f[:])
-        bn = held.tile([LANES, 4], F32, name="bn")
-        nc.vector.tensor_copy(bn[:], bn_ps[:, 0:4])
-        k_scale = held.tile([LANES, 1], F32, name="k_scale")
-        k_shift = held.tile([LANES, 1], F32, name="k_shift")
-        nc.vector.tensor_scalar_add(k_scale[:], bn[:, 3:4], BN_EPS)
-        nc.scalar.sqrt(k_scale[:], k_scale[:])
-        nc.vector.reciprocal(k_scale[:], k_scale[:])
-        nc.vector.tensor_mul(k_scale[:], k_scale[:], bn[:, 0:1])
-        nc.vector.tensor_mul(k_shift[:], bn[:, 2:3], k_scale[:])
-        nc.vector.tensor_sub(k_shift[:], bn[:, 1:2], k_shift[:])
-
+        offsets = held.tile([LANES, N // 16], U16, name="offsets")
         keys = held.tile([LANES, V], BF16, name="keys")
-        for i in range(V // BANK):
-            k_ps = psum_work.tile([LANES, BANK], F32, name="k_ps", tag="work")
-            for cb in range(CB):
-                nc.tensor.matmul(k_ps[:], weights[:, cb, :], feat[cb][:, chunk(i)], start=(cb == 0), stop=(cb == CB - 1))
-            nc.scalar.activation(keys[:, chunk(i)], k_ps[:], ACT.Identity, bias=k_shift[:], scale=k_scale[:])
-
-        keys_t = held.tile([LANES, NB, P], BF16, name="keys_t")
-        for g in range(NB // 4):
-            kt_ps = psum_work.tile([LANES, 4, P], BF16, name="kt_ps", tag="work")
-            for i in range(4):
-                nc.tensor.transpose(kt_ps[:, i, :], keys[:, block(4 * g + i)], ident_b[:])
-            nc.vector.tensor_copy(keys_t[:, 4 * g : 4 * g + 4, :], kt_ps[:])
-
-        squares = held.tile([LANES, NB, P], F32, name="squares")
-        nc.scalar.square(squares[:], keys_t[:])
-        norm = held.tile([LANES, NB], F32, name="norm")
-        nc.vector.reduce_sum(norm[:], squares[:], axis=AXIS.X)
         neg_half_norm = held.tile([LANES, NB], F32, name="neg_half_norm")
-        nc.vector.tensor_scalar_mul(neg_half_norm[:], norm[:], -0.5)
-        exp_bias = held.tile([LANES, NB], F32, name="exp_bias")
-        nc.vector.tensor_scalar_mul(exp_bias[:], norm[:], -1.0 / TEMPERATURE)
-
         feat_t = held.tile([LANES, NB, CB, LANES], BF16, name="feat_t")
-        for nb in range(NB):
-            ft_ps = psum_work.tile([LANES, CB, LANES], BF16, name="ft_ps", tag="work")
-            for cb in range(CB):
-                nc.tensor.transpose(ft_ps[:, cb, :], feat[cb][:, block(nb)], ident_b[:])
-            if nb % 2 == 0:
-                nc.scalar.copy(feat_t[:, nb, :, :], ft_ps[:])
-            else:
-                nc.vector.tensor_copy(feat_t[:, nb, :, :], ft_ps[:])
-
         proto = held.tile([LANES, N], BF16, name="proto")
-        proto_ps = [psum_long.tile([LANES, BANK], F32, name=f"proto_ps{jc}", tag="long") for jc in range(JC)]
-        for nb in range(NB):
-            for jc in range(JC):
-                nc.tensor.matmul(
-                    proto_ps[jc][:], keys_t[:, nb, :], member[:, nb, chunk(jc)], start=(nb == 0), stop=(nb == NB - 1)
-                )
-        for jc in range(JC):
-            nc.vector.tensor_tensor(proto[:, chunk(jc)], proto_ps[jc][:], deg[:, chunk(jc)], ALU.mult)
-
-        lane_max = [held.tile([LANES, BANK], F32, name=f"lane_max{jc}") for jc in range(JC)]
-        shift = [held.tile([LANES, BANK], BF16, name=f"shift{jc}") for jc in range(JC)]
+        deg = held.tile([LANES, N], F32, name="deg")
+        y = [held.tile([LANES, NB, BANK], F32, name=f"y{jc}") for jc in range(JC)]
         soft = [held.tile([LANES, NB, BANK], BF16, name=f"soft{jc}") for jc in range(JC)]
+        lane_max = [held.tile([LANES, BANK], F32, name=f"lane_max{jc}") for jc in range(JC)]
+        lane_top = [held.tile([LANES, BANK], BF16, name=f"lane_top{jc}") for jc in range(JC)]
+        neg_top = [held.tile([LANES, BANK], F32, name=f"neg_top{jc}") for jc in range(JC)]
+        factor = [held.tile([LANES, BANK], F32, name=f"factor{jc}") for jc in range(JC)]
 
-        def inner_products(jc, nb, closed):
-            z_ps = psum_work.tile([LANES, BANK], F32, name="z_ps", tag="work")
-            nc.tensor.matmul(z_ps[:], keys[:, block(nb)], proto[:, chunk(jc)], start=True, stop=closed)
-            return z_ps
+        def scores(jc, nb):
+            y_ps = psum_work.tile([LANES, BANK], F32, name="y_ps", tag="work")
+            nc.tensor.matmul(y_ps[:], keys[:, block(nb)], proto[:, chunk(jc)], start=True, stop=True)
+            nc.scalar.activation(y[jc][:, nb, :], y_ps[:], ACT.Identity, bias=neg_half_norm[:, nb : nb + 1])
+            if nb == 1:
+                nc.vector.tensor_tensor(lane_max[jc][:], y[jc][:, 0, :], y[jc][:, 1, :], ALU.max)
+            elif nb == NB - 1:
+                nc.vector.tensor_tensor(lane_top[jc][:], lane_max[jc][:], y[jc][:, nb, :], ALU.max)
+            elif nb > 1:
+                nc.vector.tensor_tensor(lane_max[jc][:], lane_max[jc][:], y[jc][:, nb, :], ALU.max)
 
-        def first_pass(jc, nb):
-            z_ps = inner_products(jc, nb, True)
-            if nb == 0:
-                nc.vector.tensor_scalar_add(lane_max[jc][:], z_ps[:], neg_half_norm[:, 0:1])
-            else:
-                nc.vector.scalar_tensor_tensor(
-                    lane_max[jc][:], z_ps[:], neg_half_norm[:, nb : nb + 1], lane_max[jc][:], ALU.add, ALU.max
-                )
+        def spread(column, ones, name):
+            diagonal = held.tile([LANES, BANK], ones.dtype, name="diagonal_" + name)
+            for q in range(QUARTERS):
+                nc.vector.tensor_scalar_mul(diagonal[:, block(q)], ident_f[:], column[:, q : q + 1])
+            spread_ps = psum_small.tile([LANES, BANK], F32, name="spread_ps", tag="spread")
+            nc.tensor.matmul(spread_ps[:], ones[:], diagonal[:], start=True, stop=True)
+            return spread_ps
 
         def maximum_over_lanes(jc):
-            lanes_ps = psum_work.tile([LANES, QUARTERS, LANES], F32, name="lanes_ps", tag="work")
+            lanes_ps = psum_small.tile([LANES, QUARTERS, LANES], BF16, name="lanes_ps", tag="column")
             for q in range(QUARTERS):
-                nc.tensor.transpose(lanes_ps[:, q, :], lane_max[jc][:, block(q)], ident_f[:])
-            neg_top = held.tile([LANES, QUARTERS], F32, name=f"neg_top{jc}")
-            nc.vector.tensor_reduce(neg_top[:], lanes_ps[:], axis=AXIS.X, op=ALU.max, negate=True)
-            for q in range(QUARTERS):
-                nc.vector.tensor_scalar_mul(shift[jc][:, block(q)], ident_f[:], neg_top[:, q : q + 1])
+                nc.tensor.transpose(lanes_ps[:, q, :], lane_top[jc][:, block(q)], ident_b[:])
+            column = held.tile([LANES, QUARTERS], F32, name=f"neg_top_column{jc}")
+            nc.vector.tensor_reduce(column[:], lanes_ps[:], axis=AXIS.X, op=ALU.max, negate=True)
+            nc.vector.tensor_copy(neg_top[jc][:], spread(column, ones_b, f"top{jc}")[:])
 
-        def second_pass(jc, nb):
-            z_ps = inner_products(jc, nb, False)
-            nc.tensor.matmul(z_ps[:], ones_b[:], shift[jc][:], start=False, stop=True)
-            nc.scalar.activation(
-                soft[jc][:, nb, :], z_ps[:], ACT.Exp, bias=exp_bias[:, nb : nb + 1], scale=2.0 / TEMPERATURE
-            )
+        def exponentials(jc, g):
+            half = GROUP // 2
+            shift = neg_top[jc][:].unsqueeze(1).to_broadcast([LANES, half, BANK])
+            first = y[jc][:, g * GROUP : g * GROUP + half, :]
+            second = y[jc][:, g * GROUP + half : (g + 1) * GROUP, :]
+            nc.vector.tensor_tensor(first, first, shift, ALU.add)
+            nc.gpsimd.tensor_tensor(second, second, shift, ALU.add)
+            nc.scalar.activation(soft[jc][:, group(g), :], y[jc][:, group(g), :], ACT.Exp, scale=2.0 / TEMPERATURE)
 
         def last_factor(jc):
-            sum_ps = psum_small.tile([LANES, QUARTERS], F32, name="sum_ps")
+            sum_ps = psum_small.tile([LANES, QUARTERS], F32, name="sum_ps", tag="column")
             for q in range(QUARTERS):
                 for nb in range(NB):
                     nc.tensor.matmul(
@@ -175,34 +114,109 @@ def tile_whnnaggregator_b_kernel(
                     )
             inv_sum = held.tile([LANES, QUARTERS], F32, name=f"inv_sum{jc}")
             nc.vector.reciprocal(inv_sum[:], sum_ps[:])
-            diagonal = held.tile([LANES, BANK], F32, name=f"diagonal{jc}")
-            for q in range(QUARTERS):
-                nc.vector.tensor_scalar_mul(diagonal[:, block(q)], ident_f[:], inv_sum[:, q : q + 1])
-            spread_ps = psum_small.tile([LANES, BANK], F32, name="spread_ps")
-            nc.tensor.matmul(spread_ps[:], ones_f[:], diagonal[:], start=True, stop=True)
-            factor = held.tile([LANES, BANK], F32, name=f"factor{jc}")
-            nc.vector.tensor_tensor(factor[:], spread_ps[:], deg[:, chunk(jc)], ALU.mult)
-            return factor
+            nc.vector.tensor_tensor(factor[jc][:], spread(inv_sum, ones_f, f"sum{jc}")[:], deg[:, chunk(jc)], ALU.mult)
 
-        for nb in range(NB):
-            first_pass(0, nb)
-        for jc in range(JC):
-            maximum_over_lanes(jc)
-            for nb in range(NB):
-                if jc + 1 < JC:
-                    first_pass(jc + 1, nb)
-                second_pass(jc, nb)
-            factor = last_factor(jc)
+        with tc.tile_pool(name="early", bufs=1) as early:
+            bn_rows = early.tile([LANES, LANES], F32, name="bn_rows")
+            nc.vector.memset(bn_rows[:], 0.0)
+            for row, vector in enumerate((bn_gamma, bn_beta, bn_mean, bn_var)):
+                queues[row % 2].dma_start(bn_rows[row : row + 1, :], vector.rearrange("p one -> one p"))
 
-            piece = offsets[:, jc * (BANK // 16) : (jc + 1) * (BANK // 16)]
-            for cb in range(CB):
-                agg_ps = psum_long.tile([LANES, BANK], F32, name="agg_ps", tag="long")
+            weights = early.tile([LANES, CB, P], BF16, name="weights")
+            nc.sync.dma_start(weights[:], proj_w.rearrange("(cb c) p -> c cb p", c=LANES))
+
+            feat = [early.tile([LANES, V], BF16, name=f"feat{cb}") for cb in range(CB)]
+            for half in (slice(0, V // 2), slice(V // 2, V)):
+                for cb in range(CB):
+                    queues[cb % 2].dma_start(feat[cb][:, half], vertex_feat[block(cb), half])
+
+            member = early.tile([LANES, NB, N], BF16, name="member")
+            incidence_blocks = incidence.rearrange("(nb n) j -> n nb j", n=LANES)
+            for g in range(NB // GROUP):
+                queues[g % 2].dma_start(member[:, group(g), chunk(0)], incidence_blocks[:, group(g), chunk(0)])
+            nc.scalar.dma_start(deg[:], inv_deg[0, :].partition_broadcast(LANES))
+            nc.sync.dma_start(offsets[:], offs)
+            for g in range(NB // GROUP):
+                queues[g % 2].dma_start(member[:, group(g), chunk(1)], incidence_blocks[:, group(g), chunk(1)])
+
+            bn_ps = psum_small.tile([LANES, LANES], F32, name="bn_ps", tag="column")
+            nc.tensor.transpose(bn_ps[:], bn_rows[:], ident_f[:])
+            bn = early.tile([LANES, 4], F32, name="bn")
+            nc.vector.tensor_copy(bn[:], bn_ps[:, 0:4])
+            k_scale = early.tile([LANES, 1], F32, name="k_scale")
+            k_shift = early.tile([LANES, 1], F32, name="k_shift")
+            nc.vector.tensor_scalar_add(k_scale[:], bn[:, 3:4], BN_EPS)
+            nc.scalar.activation(k_scale[:], k_scale[:], ACT.Ln)
+            nc.scalar.activation(k_scale[:], k_scale[:], ACT.Exp, scale=-0.5)
+            nc.vector.tensor_mul(k_scale[:], k_scale[:], bn[:, 0:1])
+            nc.vector.tensor_mul(k_shift[:], bn[:, 2:3], k_scale[:])
+            nc.vector.tensor_sub(k_shift[:], bn[:, 1:2], k_shift[:])
+
+            keys_t = early.tile([LANES, NB, P], BF16, name="keys_t")
+            half_squares = early.tile([LANES, NB, P], F32, name="half_squares")
+            for g in range(NB // GROUP):
+                k_ps = psum_work.tile([LANES, BANK], F32, name="k_ps", tag="work")
+                for cb in range(CB):
+                    nc.tensor.matmul(
+                        k_ps[:], weights[:, cb, :], feat[cb][:, chunk(g)], start=(cb == 0), stop=(cb == CB - 1)
+                    )
+                nc.scalar.activation(keys[:, chunk(g)], k_ps[:], ACT.Identity, bias=k_shift[:], scale=k_scale[:])
+                kt_ps = psum_work.tile([LANES, GROUP, P], BF16, name="kt_ps", tag="work")
+                for i in range(GROUP):
+                    nc.tensor.transpose(kt_ps[:, i, :], keys[:, block(g * GROUP + i)], ident_b[:])
+                nc.vector.tensor_copy(keys_t[:, group(g), :], kt_ps[:])
+                nc.scalar.activation(half_squares[:, group(g), :], keys_t[:, group(g), :], ACT.Square, scale=math.sqrt(0.5))
+                nc.vector.tensor_reduce(
+                    neg_half_norm[:, group(g)], half_squares[:, group(g), :], axis=AXIS.X, op=ALU.add, negate=True
+                )
+
+            def prototypes(jc):
+                proto_ps = psum_long.tile([LANES, BANK], F32, name="proto_ps", tag="long")
                 for nb in range(NB):
                     nc.tensor.matmul(
-                        agg_ps[:], feat_t[:, nb, cb, :], soft[jc][:, nb, :], start=(nb == 0), stop=(nb == NB - 1)
+                        proto_ps[:], keys_t[:, nb, :], member[:, nb, chunk(jc)], start=(nb == 0), stop=(nb == NB - 1)
                     )
-                agg = ring.tile([LANES, BANK], F32, name="agg")
-                nc.scalar.copy(agg[:], agg_ps[:])
-                nc.vector.tensor_tensor(window[cb][:].indirect(piece), agg[:], factor[:], ALU.mult)
-                if jc == JC - 1:
-                    queues[cb % 2].dma_start(out[block(cb), :], window[cb][:])
+                nc.vector.tensor_tensor(proto[:, chunk(jc)], proto_ps[:], deg[:, chunk(jc)], ALU.mult)
+
+            prototypes(0)
+            for nb in range(NB):
+                scores(0, nb)
+            prototypes(1)
+            for nb in range(NB):
+                ft_ps = psum_long.tile([LANES, CB, LANES], BF16, name="ft_ps", tag="long")
+                for cb in range(CB):
+                    nc.tensor.transpose(ft_ps[:, cb, :], feat[cb][:, block(nb)], ident_b[:])
+                if nb % 2 == 0:
+                    nc.scalar.copy(feat_t[:, nb, :, :], ft_ps[:])
+                else:
+                    nc.vector.tensor_copy(feat_t[:, nb, :, :], ft_ps[:])
+
+        with tc.tile_pool(name="late", bufs=1) as late:
+            window = [late.tile([LANES, S], F32, name=f"window{cb}") for cb in range(CB)]
+            for cb in range(CB):
+                nc.sync.dma_start(window[cb][:], base[block(cb), :])
+
+            for jc in range(JC):
+                if jc > 0:
+                    for nb in range(NB):
+                        scores(jc, nb)
+                maximum_over_lanes(jc)
+                for g in range(NB // GROUP):
+                    exponentials(jc, g)
+                last_factor(jc)
+
+            for jc in range(JC):
+                piece = offsets[:, jc * (BANK // 16) : (jc + 1) * (BANK // 16)]
+                for together in ((0, 1), (2,), (3,)):
+                    agg_ps = {cb: psum_long.tile([LANES, BANK], F32, name=f"agg_ps{cb}", tag="long") for cb in together}
+                    for nb in range(NB):
+                        for cb in together:
+                            nc.tensor.matmul(
+                                agg_ps[cb][:], feat_t[:, nb, cb, :], soft[jc][:, nb, :], start=(nb == 0), stop=(nb == NB - 1)
+                            )
+                    for cb in together:
+                        agg = ring.tile([LANES, BANK], F32, name="agg")
+                        nc.scalar.copy(agg[:], agg_ps[cb][:])
+                        nc.vector.tensor_tensor(window[cb][:].indirect(piece), agg[:], factor[jc][:], ALU.mult)
+                        if jc == JC - 1:
+                            queues[cb % 2].dma_start(out[block(cb), :], window[cb][:])

@@ -20,6 +20,7 @@ NB = V // LANES
 JC = N // BANK
 QUARTERS = BANK // LANES
 GROUP = 4
+PAIR = 2
 
 
 def block(i):
@@ -66,7 +67,6 @@ def tile_whnnaggregator_b_kernel(
         soft = [held.tile([LANES, NB, BANK], BF16, name=f"soft{jc}") for jc in range(JC)]
         lane_max = [held.tile([LANES, BANK], F32, name=f"lane_max{jc}") for jc in range(JC)]
         lane_top = [held.tile([LANES, BANK], BF16, name=f"lane_top{jc}") for jc in range(JC)]
-        neg_top = [held.tile([LANES, BANK], F32, name=f"neg_top{jc}") for jc in range(JC)]
         factor = [held.tile([LANES, BANK], F32, name=f"factor{jc}") for jc in range(JC)]
 
         def scores(jc, nb):
@@ -94,16 +94,13 @@ def tile_whnnaggregator_b_kernel(
                 nc.tensor.transpose(lanes_ps[:, q, :], lane_top[jc][:, block(q)], ident_b[:])
             column = held.tile([LANES, QUARTERS], F32, name=f"neg_top_column{jc}")
             nc.vector.tensor_reduce(column[:], lanes_ps[:], axis=AXIS.X, op=ALU.max, negate=True)
-            nc.vector.tensor_copy(neg_top[jc][:], spread(column, ones_b, f"top{jc}")[:])
+            return spread(column, ones_b, f"top{jc}")
 
-        def exponentials(jc, g):
-            half = GROUP // 2
-            shift = neg_top[jc][:].unsqueeze(1).to_broadcast([LANES, half, BANK])
-            first = y[jc][:, g * GROUP : g * GROUP + half, :]
-            second = y[jc][:, g * GROUP + half : (g + 1) * GROUP, :]
-            nc.vector.tensor_tensor(first, first, shift, ALU.add)
-            nc.gpsimd.tensor_tensor(second, second, shift, ALU.add)
-            nc.scalar.activation(soft[jc][:, group(g), :], y[jc][:, group(g), :], ACT.Exp, scale=2.0 / TEMPERATURE)
+        def exponentials(jc, first, neg_top_ps):
+            pair = slice(first, first + PAIR)
+            shift = neg_top_ps[:].unsqueeze(1).to_broadcast([LANES, PAIR, BANK])
+            nc.vector.tensor_tensor(y[jc][:, pair, :], y[jc][:, pair, :], shift, ALU.add)
+            nc.scalar.activation(soft[jc][:, pair, :], y[jc][:, pair, :], ACT.Exp, scale=2.0 / TEMPERATURE)
 
         def last_factor(jc):
             sum_ps = psum_small.tile([LANES, QUARTERS], F32, name="sum_ps", tag="column")
@@ -117,40 +114,33 @@ def tile_whnnaggregator_b_kernel(
             nc.vector.tensor_tensor(factor[jc][:], spread(inv_sum, ones_f, f"sum{jc}")[:], deg[:, chunk(jc)], ALU.mult)
 
         with tc.tile_pool(name="early", bufs=1) as early:
-            bn_rows = early.tile([LANES, LANES], F32, name="bn_rows")
-            nc.vector.memset(bn_rows[:], 0.0)
-            for row, vector in enumerate((bn_gamma, bn_beta, bn_mean, bn_var)):
-                queues[row % 2].dma_start(bn_rows[row : row + 1, :], vector.rearrange("p one -> one p"))
-
             weights = early.tile([LANES, CB, P], BF16, name="weights")
-            nc.sync.dma_start(weights[:], proj_w.rearrange("(cb c) p -> c cb p", c=LANES))
+            nc.scalar.dma_start(weights[:], proj_w.rearrange("(cb c) p -> c cb p", c=LANES))
+            feat = early.tile([LANES, CB, V], BF16, name="feat")
+            feat_blocks = vertex_feat.rearrange("(cb c) n -> c cb n", c=LANES)
+            for g in range(NB // GROUP):
+                nc.scalar.dma_start(feat[:, :, chunk(g)], feat_blocks[:, :, chunk(g)])
 
-            feat = [early.tile([LANES, V], BF16, name=f"feat{cb}") for cb in range(CB)]
-            for half in (slice(0, V // 2), slice(V // 2, V)):
-                for cb in range(CB):
-                    queues[cb % 2].dma_start(feat[cb][:, half], vertex_feat[block(cb), half])
+            var = early.tile([LANES, 1], F32, name="var")
+            gamma = early.tile([LANES, 1], F32, name="gamma")
+            mean = early.tile([LANES, 1], F32, name="mean")
+            beta = early.tile([LANES, 1], F32, name="beta")
+            for column, vector in ((var, bn_var), (gamma, bn_gamma), (mean, bn_mean), (beta, bn_beta)):
+                nc.sync.dma_start(column[:], vector)
 
             member = early.tile([LANES, NB, N], BF16, name="member")
             incidence_blocks = incidence.rearrange("(nb n) j -> n nb j", n=LANES)
-            for g in range(NB // GROUP):
-                queues[g % 2].dma_start(member[:, group(g), chunk(0)], incidence_blocks[:, group(g), chunk(0)])
-            nc.scalar.dma_start(deg[:], inv_deg[0, :].partition_broadcast(LANES))
+            nc.sync.dma_start(member[:, :, chunk(0)], incidence_blocks[:, :, chunk(0)])
+            nc.sync.dma_start(deg[:], inv_deg[0, :].partition_broadcast(LANES))
             nc.sync.dma_start(offsets[:], offs)
-            for g in range(NB // GROUP):
-                queues[g % 2].dma_start(member[:, group(g), chunk(1)], incidence_blocks[:, group(g), chunk(1)])
+            nc.sync.dma_start(member[:, :, chunk(1)], incidence_blocks[:, :, chunk(1)])
 
-            bn_ps = psum_small.tile([LANES, LANES], F32, name="bn_ps", tag="column")
-            nc.tensor.transpose(bn_ps[:], bn_rows[:], ident_f[:])
-            bn = early.tile([LANES, 4], F32, name="bn")
-            nc.vector.tensor_copy(bn[:], bn_ps[:, 0:4])
             k_scale = early.tile([LANES, 1], F32, name="k_scale")
             k_shift = early.tile([LANES, 1], F32, name="k_shift")
-            nc.vector.tensor_scalar_add(k_scale[:], bn[:, 3:4], BN_EPS)
-            nc.scalar.activation(k_scale[:], k_scale[:], ACT.Ln)
-            nc.scalar.activation(k_scale[:], k_scale[:], ACT.Exp, scale=-0.5)
-            nc.vector.tensor_mul(k_scale[:], k_scale[:], bn[:, 0:1])
-            nc.vector.tensor_mul(k_shift[:], bn[:, 2:3], k_scale[:])
-            nc.vector.tensor_sub(k_shift[:], bn[:, 1:2], k_shift[:])
+            nc.scalar.activation(k_scale[:], var[:], ACT.Abs_reciprocal_sqrt, bias=BN_EPS)
+            nc.vector.tensor_mul(k_scale[:], k_scale[:], gamma[:])
+            nc.vector.tensor_mul(k_shift[:], mean[:], k_scale[:])
+            nc.vector.tensor_sub(k_shift[:], beta[:], k_shift[:])
 
             keys_t = early.tile([LANES, NB, P], BF16, name="keys_t")
             half_squares = early.tile([LANES, NB, P], F32, name="half_squares")
@@ -158,13 +148,13 @@ def tile_whnnaggregator_b_kernel(
                 k_ps = psum_work.tile([LANES, BANK], F32, name="k_ps", tag="work")
                 for cb in range(CB):
                     nc.tensor.matmul(
-                        k_ps[:], weights[:, cb, :], feat[cb][:, chunk(g)], start=(cb == 0), stop=(cb == CB - 1)
+                        k_ps[:], weights[:, cb, :], feat[:, cb, chunk(g)], start=(cb == 0), stop=(cb == CB - 1)
                     )
-                nc.scalar.activation(keys[:, chunk(g)], k_ps[:], ACT.Identity, bias=k_shift[:], scale=k_scale[:])
+                nc.vector.tensor_scalar(keys[:, chunk(g)], k_ps[:], k_scale[:], k_shift[:], ALU.mult, ALU.add)
                 kt_ps = psum_work.tile([LANES, GROUP, P], BF16, name="kt_ps", tag="work")
                 for i in range(GROUP):
                     nc.tensor.transpose(kt_ps[:, i, :], keys[:, block(g * GROUP + i)], ident_b[:])
-                nc.vector.tensor_copy(keys_t[:, group(g), :], kt_ps[:])
+                nc.scalar.copy(keys_t[:, group(g), :], kt_ps[:])
                 nc.scalar.activation(half_squares[:, group(g), :], keys_t[:, group(g), :], ACT.Square, scale=math.sqrt(0.5))
                 nc.vector.tensor_reduce(
                     neg_half_norm[:, group(g)], half_squares[:, group(g), :], axis=AXIS.X, op=ALU.add, negate=True
@@ -185,7 +175,7 @@ def tile_whnnaggregator_b_kernel(
             for nb in range(NB):
                 ft_ps = psum_long.tile([LANES, CB, LANES], BF16, name="ft_ps", tag="long")
                 for cb in range(CB):
-                    nc.tensor.transpose(ft_ps[:, cb, :], feat[cb][:, block(nb)], ident_b[:])
+                    nc.tensor.transpose(ft_ps[:, cb, :], feat[:, cb, block(nb)], ident_b[:])
                 if nb % 2 == 0:
                     nc.scalar.copy(feat_t[:, nb, :, :], ft_ps[:])
                 else:
@@ -200,9 +190,9 @@ def tile_whnnaggregator_b_kernel(
                 if jc > 0:
                     for nb in range(NB):
                         scores(jc, nb)
-                maximum_over_lanes(jc)
-                for g in range(NB // GROUP):
-                    exponentials(jc, g)
+                neg_top_ps = maximum_over_lanes(jc)
+                for first in range(0, NB, PAIR):
+                    exponentials(jc, first, neg_top_ps)
                 last_factor(jc)
 
             for jc in range(JC):

@@ -20,7 +20,6 @@ NB = V // LANES
 JC = N // BANK
 QUARTERS = BANK // LANES
 GROUP = 4
-PAIR = 2
 
 
 def block(i):
@@ -59,26 +58,19 @@ def tile_whnnaggregator_b_kernel(
 
         offsets = held.tile([LANES, N // 16], U16, name="offsets")
         keys = held.tile([LANES, V], BF16, name="keys")
-        neg_half_norm = held.tile([LANES, NB], F32, name="neg_half_norm")
+        neg_norm = held.tile([LANES, NB], F32, name="neg_norm")
         feat_t = held.tile([LANES, NB, CB, LANES], BF16, name="feat_t")
         proto = held.tile([LANES, N], BF16, name="proto")
         deg = held.tile([LANES, N], F32, name="deg")
-        y = [held.tile([LANES, NB, BANK], F32, name=f"y{jc}") for jc in range(JC)]
         soft = [held.tile([LANES, NB, BANK], BF16, name=f"soft{jc}") for jc in range(JC)]
-        lane_max = [held.tile([LANES, BANK], F32, name=f"lane_max{jc}") for jc in range(JC)]
-        lane_top = [held.tile([LANES, BANK], BF16, name=f"lane_top{jc}") for jc in range(JC)]
         factor = [held.tile([LANES, BANK], F32, name=f"factor{jc}") for jc in range(JC)]
 
-        def scores(jc, nb):
-            y_ps = psum_work.tile([LANES, BANK], F32, name="y_ps", tag="work")
-            nc.tensor.matmul(y_ps[:], keys[:, block(nb)], proto[:, chunk(jc)], start=True, stop=True)
-            nc.scalar.activation(y[jc][:, nb, :], y_ps[:], ACT.Identity, bias=neg_half_norm[:, nb : nb + 1])
-            if nb == 1:
-                nc.vector.tensor_tensor(lane_max[jc][:], y[jc][:, 0, :], y[jc][:, 1, :], ALU.max)
-            elif nb == NB - 1:
-                nc.vector.tensor_tensor(lane_top[jc][:], lane_max[jc][:], y[jc][:, nb, :], ALU.max)
-            elif nb > 1:
-                nc.vector.tensor_tensor(lane_max[jc][:], lane_max[jc][:], y[jc][:, nb, :], ALU.max)
+        def weights_of(jc, nb):
+            dot_ps = psum_work.tile([LANES, BANK], F32, name="dot_ps", tag="work")
+            nc.tensor.matmul(dot_ps[:], keys[:, block(nb)], proto[:, chunk(jc)], start=True, stop=True)
+            nc.scalar.activation(
+                soft[jc][:, nb, :], dot_ps[:], ACT.Exp, bias=neg_norm[:, nb : nb + 1], scale=2.0 / TEMPERATURE
+            )
 
         def spread(column, ones, name):
             diagonal = held.tile([LANES, BANK], ones.dtype, name="diagonal_" + name)
@@ -87,20 +79,6 @@ def tile_whnnaggregator_b_kernel(
             spread_ps = psum_small.tile([LANES, BANK], F32, name="spread_ps", tag="spread")
             nc.tensor.matmul(spread_ps[:], ones[:], diagonal[:], start=True, stop=True)
             return spread_ps
-
-        def maximum_over_lanes(jc):
-            lanes_ps = psum_small.tile([LANES, QUARTERS, LANES], BF16, name="lanes_ps", tag="column")
-            for q in range(QUARTERS):
-                nc.tensor.transpose(lanes_ps[:, q, :], lane_top[jc][:, block(q)], ident_b[:])
-            column = held.tile([LANES, QUARTERS], F32, name=f"neg_top_column{jc}")
-            nc.vector.tensor_reduce(column[:], lanes_ps[:], axis=AXIS.X, op=ALU.max, negate=True)
-            return spread(column, ones_b, f"top{jc}")
-
-        def exponentials(jc, first, neg_top_ps):
-            pair = slice(first, first + PAIR)
-            shift = neg_top_ps[:].unsqueeze(1).to_broadcast([LANES, PAIR, BANK])
-            nc.vector.tensor_tensor(y[jc][:, pair, :], y[jc][:, pair, :], shift, ALU.add)
-            nc.scalar.activation(soft[jc][:, pair, :], y[jc][:, pair, :], ACT.Exp, scale=2.0 / TEMPERATURE)
 
         def last_factor(jc):
             sum_ps = psum_small.tile([LANES, QUARTERS], F32, name="sum_ps", tag="column")
@@ -143,7 +121,7 @@ def tile_whnnaggregator_b_kernel(
             nc.vector.tensor_sub(k_shift[:], beta[:], k_shift[:])
 
             keys_t = early.tile([LANES, NB, P], BF16, name="keys_t")
-            half_squares = early.tile([LANES, NB, P], F32, name="half_squares")
+            squares = early.tile([LANES, NB, P], F32, name="squares")
             for g in range(NB // GROUP):
                 k_ps = psum_work.tile([LANES, BANK], F32, name="k_ps", tag="work")
                 for cb in range(CB):
@@ -155,10 +133,10 @@ def tile_whnnaggregator_b_kernel(
                 for i in range(GROUP):
                     nc.tensor.transpose(kt_ps[:, i, :], keys[:, block(g * GROUP + i)], ident_b[:])
                 nc.scalar.copy(keys_t[:, group(g), :], kt_ps[:])
-                nc.scalar.activation(half_squares[:, group(g), :], keys_t[:, group(g), :], ACT.Square, scale=math.sqrt(0.5))
-                nc.vector.tensor_reduce(
-                    neg_half_norm[:, group(g)], half_squares[:, group(g), :], axis=AXIS.X, op=ALU.add, negate=True
+                nc.scalar.activation(
+                    squares[:, group(g), :], keys_t[:, group(g), :], ACT.Square, scale=math.sqrt(1.0 / TEMPERATURE)
                 )
+                nc.vector.tensor_reduce(neg_norm[:, group(g)], squares[:, group(g), :], axis=AXIS.X, op=ALU.add, negate=True)
 
             def prototypes(jc):
                 proto_ps = psum_long.tile([LANES, BANK], F32, name="proto_ps", tag="long")
@@ -170,7 +148,7 @@ def tile_whnnaggregator_b_kernel(
 
             prototypes(0)
             for nb in range(NB):
-                scores(0, nb)
+                weights_of(0, nb)
             prototypes(1)
             for nb in range(NB):
                 ft_ps = psum_long.tile([LANES, CB, LANES], BF16, name="ft_ps", tag="long")
@@ -186,14 +164,10 @@ def tile_whnnaggregator_b_kernel(
             for cb in range(CB):
                 nc.sync.dma_start(window[cb][:], base[block(cb), :])
 
-            for jc in range(JC):
-                if jc > 0:
-                    for nb in range(NB):
-                        scores(jc, nb)
-                neg_top_ps = maximum_over_lanes(jc)
-                for first in range(0, NB, PAIR):
-                    exponentials(jc, first, neg_top_ps)
-                last_factor(jc)
+            last_factor(0)
+            for nb in range(NB):
+                weights_of(1, nb)
+            last_factor(1)
 
             for jc in range(JC):
                 piece = offsets[:, jc * (BANK // 16) : (jc + 1) * (BANK // 16)]

@@ -20,6 +20,8 @@ NB = V // LANES
 JC = N // BANK
 QUARTERS = BANK // LANES
 GROUP = 4
+PAIR = 2
+LEAD = 4
 
 
 def block(i):
@@ -40,12 +42,32 @@ def tile_whnnaggregator_b_kernel(
     nc = tc.nc
     with (
         tc.tile_pool(name="held", bufs=1) as held,
-        tc.tile_pool(name="ring", bufs=2) as ring,
         tc.psum_pool(name="psum_work", bufs=3) as psum_work,
         tc.psum_pool(name="psum_long", bufs=3) as psum_long,
         tc.psum_pool(name="psum_small", bufs=1) as psum_small,
     ):
-        queues = (nc.sync, nc.scalar)
+        feat = held.tile([LANES, CB, V], BF16, name="feat")
+        feat_blocks = vertex_feat.rearrange("(cb c) n -> c cb n", c=LANES)
+        for g in range(NB // GROUP):
+            nc.sync.dma_start(feat[:, :, chunk(g)], feat_blocks[:, :, chunk(g)])
+        member = held.tile([LANES, NB, N], BF16, name="member")
+        incidence_blocks = incidence.rearrange("(nb n) j -> n nb j", n=LANES)
+        offsets = held.tile([LANES, N // 16], U16, name="offsets")
+        nc.sync.dma_start(member[:, :, chunk(0)], incidence_blocks[:, :, chunk(0)])
+        nc.sync.dma_start(offsets[:], offs)
+        nc.sync.dma_start(member[:, :, chunk(1)], incidence_blocks[:, :, chunk(1)])
+        window = [held.tile([LANES, S], F32, name=f"window{cb}") for cb in range(CB)]
+        for cb in range(CB):
+            nc.sync.dma_start(window[cb][:], base[block(cb), :])
+
+        weights = held.tile([LANES, CB, P], BF16, name="weights")
+        nc.scalar.dma_start(weights[:], proj_w.rearrange("(cb c) p -> c cb p", c=LANES))
+        var = held.tile([LANES, 1], F32, name="var")
+        gamma = held.tile([LANES, 1], F32, name="gamma")
+        mean = held.tile([LANES, 1], F32, name="mean")
+        beta = held.tile([LANES, 1], F32, name="beta")
+        for column, vector in ((var, bn_var), (gamma, bn_gamma), (mean, bn_mean), (beta, bn_beta)):
+            nc.scalar.dma_start(column[:], vector)
 
         ident_f = held.tile([LANES, LANES], F32, name="ident_f")
         make_identity(nc, ident_f[:])
@@ -55,15 +77,52 @@ def tile_whnnaggregator_b_kernel(
         nc.vector.memset(ones_b[:], 1.0)
         ones_f = held.tile([LANES, LANES], F32, name="ones_f")
         nc.vector.memset(ones_f[:], 1.0)
+        deg = held.tile([LANES, N], F32, name="deg")
+        nc.gpsimd.dma_start(deg[:], inv_deg[0, :].partition_broadcast(LANES))
 
-        offsets = held.tile([LANES, N // 16], U16, name="offsets")
         keys = held.tile([LANES, V], BF16, name="keys")
+        keys_t = held.tile([LANES, NB, P], BF16, name="keys_t")
+        squares = held.tile([LANES, NB, P], F32, name="squares")
         neg_norm = held.tile([LANES, NB], F32, name="neg_norm")
         feat_t = held.tile([LANES, NB, CB, LANES], BF16, name="feat_t")
         proto = held.tile([LANES, N], BF16, name="proto")
-        deg = held.tile([LANES, N], F32, name="deg")
         soft = [held.tile([LANES, NB, BANK], BF16, name=f"soft{jc}") for jc in range(JC)]
         factor = [held.tile([LANES, BANK], F32, name=f"factor{jc}") for jc in range(JC)]
+
+
+        k_scale = held.tile([LANES, 1], F32, name="k_scale")
+        k_shift = held.tile([LANES, 1], F32, name="k_shift")
+        nc.scalar.activation(k_scale[:], var[:], ACT.Abs_reciprocal_sqrt, bias=BN_EPS)
+        nc.vector.tensor_mul(k_scale[:], k_scale[:], gamma[:])
+        nc.vector.tensor_mul(k_shift[:], mean[:], k_scale[:])
+        nc.vector.tensor_sub(k_shift[:], beta[:], k_shift[:])
+
+        def keys_of(g):
+            k_ps = psum_work.tile([LANES, BANK], F32, name="k_ps", tag="work")
+            for cb in range(CB):
+                nc.tensor.matmul(k_ps[:], weights[:, cb, :], feat[:, cb, chunk(g)], start=(cb == 0), stop=(cb == CB - 1))
+            nc.vector.tensor_scalar(keys[:, chunk(g)], k_ps[:], k_scale[:], k_shift[:], ALU.mult, ALU.add)
+
+        def keys_transposed(g):
+            kt_ps = psum_work.tile([LANES, GROUP, P], BF16, name="kt_ps", tag="work")
+            for i in range(GROUP):
+                nc.tensor.transpose(kt_ps[:, i, :], keys[:, block(g * GROUP + i)], ident_b[:])
+            nc.scalar.copy(keys_t[:, group(g), :], kt_ps[:])
+
+        def features_transposed(first, copy):
+            ft_ps = psum_long.tile([LANES, PAIR, CB, LANES], BF16, name="ft_ps", tag="long")
+            for i in range(PAIR):
+                for cb in range(CB):
+                    nc.tensor.transpose(ft_ps[:, i, cb, :], feat[:, cb, block(first + i)], ident_b[:])
+            copy(feat_t[:, first : first + PAIR, :, :], ft_ps[:])
+
+        for g in range(NB // GROUP):
+            keys_of(g)
+            if g > 0:
+                keys_transposed(g - 1)
+            features_transposed(g * GROUP, nc.scalar.copy)
+            features_transposed(g * GROUP + PAIR, nc.vector.tensor_copy)
+        keys_transposed(NB // GROUP - 1)
 
         def weights_of(jc, nb):
             dot_ps = psum_work.tile([LANES, BANK], F32, name="dot_ps", tag="work")
@@ -72,115 +131,83 @@ def tile_whnnaggregator_b_kernel(
                 soft[jc][:, nb, :], dot_ps[:], ACT.Exp, bias=neg_norm[:, nb : nb + 1], scale=2.0 / TEMPERATURE
             )
 
-        def spread(column, ones, name):
-            diagonal = held.tile([LANES, BANK], ones.dtype, name="diagonal_" + name)
-            for q in range(QUARTERS):
-                nc.vector.tensor_scalar_mul(diagonal[:, block(q)], ident_f[:], column[:, q : q + 1])
-            spread_ps = psum_small.tile([LANES, BANK], F32, name="spread_ps", tag="spread")
-            nc.tensor.matmul(spread_ps[:], ones[:], diagonal[:], start=True, stop=True)
-            return spread_ps
+        def feed_scalar(others):
+            number = (others - LEAD) // 2
+            if others % 2 == 0 and 0 <= number < JC * NB:
+                weights_of(number // NB, number % NB)
 
-        def last_factor(jc):
-            sum_ps = psum_small.tile([LANES, QUARTERS], F32, name="sum_ps", tag="column")
-            for q in range(QUARTERS):
-                for nb in range(NB):
-                    nc.tensor.matmul(
-                        sum_ps[:, q : q + 1], soft[jc][:, nb, block(q)], ones_b[:, 0:1], start=(nb == 0), stop=(nb == NB - 1)
-                    )
-            inv_sum = held.tile([LANES, QUARTERS], F32, name=f"inv_sum{jc}")
-            nc.vector.reciprocal(inv_sum[:], sum_ps[:])
-            nc.vector.tensor_tensor(factor[jc][:], spread(inv_sum, ones_f, f"sum{jc}")[:], deg[:, chunk(jc)], ALU.mult)
+        proto_ps = psum_long.tile([LANES, BANK], F32, name="proto_ps", tag="long")
+        for nb in range(NB):
+            nc.tensor.matmul(proto_ps[:], keys_t[:, nb, :], member[:, nb, chunk(0)], start=(nb == 0), stop=(nb == NB - 1))
+        for g in range(NB // GROUP):
+            nc.scalar.activation(
+                squares[:, group(g), :], keys_t[:, group(g), :], ACT.Square, scale=math.sqrt(1.0 / TEMPERATURE)
+            )
+            nc.vector.tensor_reduce(neg_norm[:, group(g)], squares[:, group(g), :], axis=AXIS.X, op=ALU.add, negate=True)
+        nc.vector.tensor_tensor(proto[:, chunk(0)], proto_ps[:], deg[:, chunk(0)], ALU.mult)
 
-        with tc.tile_pool(name="early", bufs=1) as early:
-            weights = early.tile([LANES, CB, P], BF16, name="weights")
-            nc.scalar.dma_start(weights[:], proj_w.rearrange("(cb c) p -> c cb p", c=LANES))
-            feat = early.tile([LANES, CB, V], BF16, name="feat")
-            feat_blocks = vertex_feat.rearrange("(cb c) n -> c cb n", c=LANES)
-            for g in range(NB // GROUP):
-                nc.scalar.dma_start(feat[:, :, chunk(g)], feat_blocks[:, :, chunk(g)])
+        others = 0
+        proto_ps = psum_long.tile([LANES, BANK], F32, name="proto_ps", tag="long")
+        for nb in range(NB):
+            nc.tensor.matmul(proto_ps[:], keys_t[:, nb, :], member[:, nb, chunk(1)], start=(nb == 0), stop=(nb == NB - 1))
+            others += 1
+            feed_scalar(others)
+        nc.vector.tensor_tensor(proto[:, chunk(1)], proto_ps[:], deg[:, chunk(1)], ALU.mult)
 
-            var = early.tile([LANES, 1], F32, name="var")
-            gamma = early.tile([LANES, 1], F32, name="gamma")
-            mean = early.tile([LANES, 1], F32, name="mean")
-            beta = early.tile([LANES, 1], F32, name="beta")
-            for column, vector in ((var, bn_var), (gamma, bn_gamma), (mean, bn_mean), (beta, bn_beta)):
-                nc.sync.dma_start(column[:], vector)
+        sum_ps = {}
+        diagonal = [held.tile([LANES, BANK], F32, name=f"diagonal{jc}") for jc in range(JC)]
 
-            member = early.tile([LANES, NB, N], BF16, name="member")
-            incidence_blocks = incidence.rearrange("(nb n) j -> n nb j", n=LANES)
-            nc.sync.dma_start(member[:, :, chunk(0)], incidence_blocks[:, :, chunk(0)])
-            nc.sync.dma_start(deg[:], inv_deg[0, :].partition_broadcast(LANES))
-            nc.sync.dma_start(offsets[:], offs)
-            nc.sync.dma_start(member[:, :, chunk(1)], incidence_blocks[:, :, chunk(1)])
-
-            k_scale = early.tile([LANES, 1], F32, name="k_scale")
-            k_shift = early.tile([LANES, 1], F32, name="k_shift")
-            nc.scalar.activation(k_scale[:], var[:], ACT.Abs_reciprocal_sqrt, bias=BN_EPS)
-            nc.vector.tensor_mul(k_scale[:], k_scale[:], gamma[:])
-            nc.vector.tensor_mul(k_shift[:], mean[:], k_scale[:])
-            nc.vector.tensor_sub(k_shift[:], beta[:], k_shift[:])
-
-            keys_t = early.tile([LANES, NB, P], BF16, name="keys_t")
-            squares = early.tile([LANES, NB, P], F32, name="squares")
-            for g in range(NB // GROUP):
-                k_ps = psum_work.tile([LANES, BANK], F32, name="k_ps", tag="work")
-                for cb in range(CB):
-                    nc.tensor.matmul(
-                        k_ps[:], weights[:, cb, :], feat[:, cb, chunk(g)], start=(cb == 0), stop=(cb == CB - 1)
-                    )
-                nc.vector.tensor_scalar(keys[:, chunk(g)], k_ps[:], k_scale[:], k_shift[:], ALU.mult, ALU.add)
-                kt_ps = psum_work.tile([LANES, GROUP, P], BF16, name="kt_ps", tag="work")
-                for i in range(GROUP):
-                    nc.tensor.transpose(kt_ps[:, i, :], keys[:, block(g * GROUP + i)], ident_b[:])
-                nc.scalar.copy(keys_t[:, group(g), :], kt_ps[:])
-                nc.scalar.activation(
-                    squares[:, group(g), :], keys_t[:, group(g), :], ACT.Square, scale=math.sqrt(1.0 / TEMPERATURE)
+        def column_sum(jc, q):
+            if q == 0:
+                sum_ps[jc] = psum_small.tile([LANES, QUARTERS], F32, name="sum_ps", tag="column")
+            for nb in range(NB):
+                nc.tensor.matmul(
+                    sum_ps[jc][:, q : q + 1], soft[jc][:, nb, block(q)], ones_b[:, 0:1], start=(nb == 0), stop=(nb == NB - 1)
                 )
-                nc.vector.tensor_reduce(neg_norm[:, group(g)], squares[:, group(g), :], axis=AXIS.X, op=ALU.add, negate=True)
+            if q == QUARTERS - 1:
+                inv_sum = held.tile([LANES, QUARTERS], F32, name=f"inv_sum{jc}")
+                nc.vector.reciprocal(inv_sum[:], sum_ps[jc][:])
+                for quarter in range(QUARTERS):
+                    nc.vector.tensor_scalar_mul(diagonal[jc][:, block(quarter)], ident_f[:], inv_sum[:, quarter : quarter + 1])
 
-            def prototypes(jc):
-                proto_ps = psum_long.tile([LANES, BANK], F32, name="proto_ps", tag="long")
-                for nb in range(NB):
+        def spread(jc):
+            spread_ps = psum_small.tile([LANES, BANK], F32, name="spread_ps", tag="spread")
+            nc.tensor.matmul(spread_ps[:], ones_f[:], diagonal[jc][:], start=True, stop=True)
+            nc.vector.tensor_tensor(factor[jc][:], spread_ps[:], deg[:, chunk(jc)], ALU.mult)
+
+        unplaced = []
+        factored = []
+
+        def place():
+            for jc, cb, agg in unplaced:
+                if jc in factored:
+                    piece = offsets[:, jc * (BANK // 16) : (jc + 1) * (BANK // 16)]
+                    nc.vector.tensor_tensor(window[cb][:].indirect(piece), agg[:], factor[jc][:], ALU.mult)
+                    if jc == JC - 1:
+                        nc.sync.dma_start(out[block(cb), :], window[cb][:])
+            still_waiting = [entry for entry in unplaced if entry[0] not in factored]
+            unplaced.clear()
+            unplaced.extend(still_waiting)
+
+        passes = ((0, (0, 1)), (0, (2,)), (0, (3,)), (1, (0,)), (1, (1,)), (1, (2,)), (1, (3,)))
+        for index, (jc, together) in enumerate(passes):
+            rider = index // 2
+            agg_ps = {cb: psum_long.tile([LANES, BANK], F32, name=f"agg_ps{cb}", tag="long") for cb in together}
+            for nb in range(NB):
+                for cb in together:
                     nc.tensor.matmul(
-                        proto_ps[:], keys_t[:, nb, :], member[:, nb, chunk(jc)], start=(nb == 0), stop=(nb == NB - 1)
+                        agg_ps[cb][:], feat_t[:, nb, cb, :], soft[jc][:, nb, :], start=(nb == 0), stop=(nb == NB - 1)
                     )
-                nc.vector.tensor_tensor(proto[:, chunk(jc)], proto_ps[:], deg[:, chunk(jc)], ALU.mult)
-
-            prototypes(0)
-            for nb in range(NB):
-                weights_of(0, nb)
-            prototypes(1)
-            for nb in range(NB):
-                ft_ps = psum_long.tile([LANES, CB, LANES], BF16, name="ft_ps", tag="long")
-                for cb in range(CB):
-                    nc.tensor.transpose(ft_ps[:, cb, :], feat[:, cb, block(nb)], ident_b[:])
-                if nb % 2 == 0:
-                    nc.scalar.copy(feat_t[:, nb, :, :], ft_ps[:])
-                else:
-                    nc.vector.tensor_copy(feat_t[:, nb, :, :], ft_ps[:])
-
-        with tc.tile_pool(name="late", bufs=1) as late:
-            window = [late.tile([LANES, S], F32, name=f"window{cb}") for cb in range(CB)]
-            for cb in range(CB):
-                nc.sync.dma_start(window[cb][:], base[block(cb), :])
-
-            last_factor(0)
-            for nb in range(NB):
-                weights_of(1, nb)
-            last_factor(1)
-
-            for jc in range(JC):
-                piece = offsets[:, jc * (BANK // 16) : (jc + 1) * (BANK // 16)]
-                for together in ((0, 1), (2,), (3,)):
-                    agg_ps = {cb: psum_long.tile([LANES, BANK], F32, name=f"agg_ps{cb}", tag="long") for cb in together}
-                    for nb in range(NB):
-                        for cb in together:
-                            nc.tensor.matmul(
-                                agg_ps[cb][:], feat_t[:, nb, cb, :], soft[jc][:, nb, :], start=(nb == 0), stop=(nb == NB - 1)
-                            )
-                    for cb in together:
-                        agg = ring.tile([LANES, BANK], F32, name="agg")
-                        nc.scalar.copy(agg[:], agg_ps[cb][:])
-                        nc.vector.tensor_tensor(window[cb][:].indirect(piece), agg[:], factor[jc][:], ALU.mult)
-                        if jc == JC - 1:
-                            queues[cb % 2].dma_start(out[block(cb), :], window[cb][:])
+                    others += 1
+                    feed_scalar(others)
+                if rider < JC and index % 2 == 0 and nb >= NB - QUARTERS:
+                    column_sum(rider, nb - (NB - QUARTERS))
+                if rider < JC and index % 2 == 1 and nb == QUARTERS - 1:
+                    spread(rider)
+                    factored.append(rider)
+                    place()
+            for cb in together:
+                agg = held.tile([LANES, BANK], F32, name=f"agg{jc}{cb}")
+                nc.scalar.copy(agg[:], agg_ps[cb][:])
+                unplaced.append((jc, cb, agg))
+            place()

@@ -22,6 +22,8 @@ QUARTERS = BANK // LANES
 GROUP = 4
 PAIR = 2
 LEAD = 4
+HALF = BANK // 2
+COVER = 9
 
 
 def block(i):
@@ -46,28 +48,32 @@ def tile_whnnaggregator_b_kernel(
         tc.psum_pool(name="psum_long", bufs=3) as psum_long,
         tc.psum_pool(name="psum_small", bufs=1) as psum_small,
     ):
+        weights = held.tile([LANES, CB, P], BF16, name="weights")
+        nc.sync.dma_start(weights[:], proj_w.rearrange("(cb c) p -> c cb p", c=LANES))
         feat = held.tile([LANES, CB, V], BF16, name="feat")
         feat_blocks = vertex_feat.rearrange("(cb c) n -> c cb n", c=LANES)
+        var = held.tile([LANES, 1], F32, name="var")
+        gamma = held.tile([LANES, 1], F32, name="gamma")
+        mean = held.tile([LANES, 1], F32, name="mean")
+        beta = held.tile([LANES, 1], F32, name="beta")
+        nc.scalar.dma_start(var[:], bn_var)
+        nc.scalar.dma_start(gamma[:], bn_gamma)
         for g in range(NB // GROUP):
             nc.sync.dma_start(feat[:, :, chunk(g)], feat_blocks[:, :, chunk(g)])
+            if g == 0:
+                nc.sync.dma_start(mean[:], bn_mean)
+                nc.sync.dma_start(beta[:], bn_beta)
         member = held.tile([LANES, NB, N], BF16, name="member")
         incidence_blocks = incidence.rearrange("(nb n) j -> n nb j", n=LANES)
         offsets = held.tile([LANES, N // 16], U16, name="offsets")
         nc.sync.dma_start(member[:, :, chunk(0)], incidence_blocks[:, :, chunk(0)])
+        deg = held.tile([LANES, N], F32, name="deg")
+        nc.sync.dma_start(deg[:], inv_deg[0, :].partition_broadcast(LANES))
         nc.sync.dma_start(offsets[:], offs)
         nc.sync.dma_start(member[:, :, chunk(1)], incidence_blocks[:, :, chunk(1)])
         window = [held.tile([LANES, S], F32, name=f"window{cb}") for cb in range(CB)]
         for cb in range(CB):
             nc.sync.dma_start(window[cb][:], base[block(cb), :])
-
-        weights = held.tile([LANES, CB, P], BF16, name="weights")
-        nc.scalar.dma_start(weights[:], proj_w.rearrange("(cb c) p -> c cb p", c=LANES))
-        var = held.tile([LANES, 1], F32, name="var")
-        gamma = held.tile([LANES, 1], F32, name="gamma")
-        mean = held.tile([LANES, 1], F32, name="mean")
-        beta = held.tile([LANES, 1], F32, name="beta")
-        for column, vector in ((var, bn_var), (gamma, bn_gamma), (mean, bn_mean), (beta, bn_beta)):
-            nc.scalar.dma_start(column[:], vector)
 
         ident_f = held.tile([LANES, LANES], F32, name="ident_f")
         make_identity(nc, ident_f[:])
@@ -77,8 +83,6 @@ def tile_whnnaggregator_b_kernel(
         nc.vector.memset(ones_b[:], 1.0)
         ones_f = held.tile([LANES, LANES], F32, name="ones_f")
         nc.vector.memset(ones_f[:], 1.0)
-        deg = held.tile([LANES, N], F32, name="deg")
-        nc.gpsimd.dma_start(deg[:], inv_deg[0, :].partition_broadcast(LANES))
 
         keys = held.tile([LANES, V], BF16, name="keys")
         keys_t = held.tile([LANES, NB, P], BF16, name="keys_t")
@@ -179,35 +183,39 @@ def tile_whnnaggregator_b_kernel(
         factored = []
 
         def place():
-            for jc, cb, agg in unplaced:
-                if jc in factored:
-                    piece = offsets[:, jc * (BANK // 16) : (jc + 1) * (BANK // 16)]
-                    nc.vector.tensor_tensor(window[cb][:].indirect(piece), agg[:], factor[jc][:], ALU.mult)
-                    if jc == JC - 1:
+            for first, width, cb, agg in unplaced:
+                if first // BANK in factored:
+                    piece = offsets[:, first // 16 : (first + width) // 16]
+                    scale = factor[first // BANK][:, first % BANK : first % BANK + width]
+                    nc.vector.tensor_tensor(window[cb][:].indirect(piece), agg[:], scale, ALU.mult)
+                    if first + width == N:
                         nc.sync.dma_start(out[block(cb), :], window[cb][:])
-            still_waiting = [entry for entry in unplaced if entry[0] not in factored]
+            still_waiting = [entry for entry in unplaced if entry[0] // BANK not in factored]
             unplaced.clear()
             unplaced.extend(still_waiting)
 
-        passes = ((0, (0, 1)), (0, (2,)), (0, (3,)), (1, (0,)), (1, (1,)), (1, (2,)), (1, (3,)))
-        for index, (jc, together) in enumerate(passes):
+        passes = [(0, BANK, (0, 1)), (0, BANK, (2,)), (0, BANK, (3,))]
+        passes.extend((BANK + half * HALF, HALF, (cb,)) for cb in range(CB) for half in range(BANK // HALF))
+        for index, (first, width, together) in enumerate(passes):
+            jc = first // BANK
+            edges = slice(first % BANK, first % BANK + width)
             rider = index // 2
             agg_ps = {cb: psum_long.tile([LANES, BANK], F32, name=f"agg_ps{cb}", tag="long") for cb in together}
             for nb in range(NB):
                 for cb in together:
                     nc.tensor.matmul(
-                        agg_ps[cb][:], feat_t[:, nb, cb, :], soft[jc][:, nb, :], start=(nb == 0), stop=(nb == NB - 1)
+                        agg_ps[cb][:, 0:width], feat_t[:, nb, cb, :], soft[jc][:, nb, edges], start=(nb == 0), stop=(nb == NB - 1)
                     )
                     others += 1
                     feed_scalar(others)
                 if rider < JC and index % 2 == 0 and nb >= NB - QUARTERS:
                     column_sum(rider, nb - (NB - QUARTERS))
-                if rider < JC and index % 2 == 1 and nb == QUARTERS - 1:
+                if rider < JC and index % 2 == 1 and nb == min(NB, COVER * BANK // width) - 1:
                     spread(rider)
                     factored.append(rider)
                     place()
             for cb in together:
-                agg = held.tile([LANES, BANK], F32, name=f"agg{jc}{cb}")
-                nc.scalar.copy(agg[:], agg_ps[cb][:])
-                unplaced.append((jc, cb, agg))
+                agg = held.tile([LANES, width], F32, name=f"agg{first}_{cb}")
+                nc.scalar.copy(agg[:], agg_ps[cb][:, 0:width])
+                unplaced.append((first, width, cb, agg))
             place()

@@ -23,7 +23,6 @@ GROUP = 4
 PAIR = 2
 LEAD = 4
 HALF = BANK // 2
-COVER = 9
 
 
 def block(i):
@@ -91,6 +90,7 @@ def tile_whnnaggregator_b_kernel(
         feat_t = held.tile([LANES, NB, CB, LANES], BF16, name="feat_t")
         proto = held.tile([LANES, N], BF16, name="proto")
         soft = [held.tile([LANES, NB, BANK], BF16, name=f"soft{jc}") for jc in range(JC)]
+        lane_sum = held.tile([LANES, BANK], F32, name="lane_sum")
         factor = [held.tile([LANES, BANK], F32, name=f"factor{jc}") for jc in range(JC)]
 
 
@@ -134,6 +134,10 @@ def tile_whnnaggregator_b_kernel(
             nc.scalar.activation(
                 soft[jc][:, nb, :], dot_ps[:], ACT.Exp, bias=neg_norm[:, nb : nb + 1], scale=2.0 / TEMPERATURE
             )
+            if jc == 0 and nb == 1:
+                nc.vector.tensor_tensor(lane_sum[:], soft[0][:, 0, :], soft[0][:, 1, :], ALU.add)
+            if jc == 0 and nb > 1:
+                nc.vector.tensor_tensor(lane_sum[:], lane_sum[:], soft[0][:, nb, :], ALU.add)
 
         def feed_scalar(others):
             number = (others - LEAD) // 2
@@ -158,48 +162,37 @@ def tile_whnnaggregator_b_kernel(
             feed_scalar(others)
         nc.vector.tensor_tensor(proto[:, chunk(1)], proto_ps[:], deg[:, chunk(1)], ALU.mult)
 
-        sum_ps = {}
-        diagonal = [held.tile([LANES, BANK], F32, name=f"diagonal{jc}") for jc in range(JC)]
 
-        def column_sum(jc, q):
-            if q == 0:
-                sum_ps[jc] = psum_small.tile([LANES, QUARTERS], F32, name="sum_ps", tag="column")
+        def first_factor():
+            total_ps = psum_small.tile([LANES, BANK], F32, name="total_ps", tag="spread")
+            nc.tensor.matmul(total_ps[:], ones_f[:], lane_sum[:], start=True, stop=True)
+            nc.vector.reciprocal(factor[0][:], total_ps[:])
+            nc.vector.tensor_tensor(factor[0][:], factor[0][:], deg[:, chunk(0)], ALU.mult)
+
+        sum_ps = psum_small.tile([LANES, QUARTERS], F32, name="sum_ps", tag="column")
+        diagonal = held.tile([LANES, BANK], F32, name="diagonal")
+
+        def column_sum(q):
             for nb in range(NB):
                 nc.tensor.matmul(
-                    sum_ps[jc][:, q : q + 1], soft[jc][:, nb, block(q)], ones_b[:, 0:1], start=(nb == 0), stop=(nb == NB - 1)
+                    sum_ps[:, q : q + 1], soft[1][:, nb, block(q)], ones_b[:, 0:1], start=(nb == 0), stop=(nb == NB - 1)
                 )
             if q == QUARTERS - 1:
-                inv_sum = held.tile([LANES, QUARTERS], F32, name=f"inv_sum{jc}")
-                nc.vector.reciprocal(inv_sum[:], sum_ps[jc][:])
+                inv_sum = held.tile([LANES, QUARTERS], F32, name="inv_sum")
+                nc.vector.reciprocal(inv_sum[:], sum_ps[:])
                 for quarter in range(QUARTERS):
-                    nc.vector.tensor_scalar_mul(diagonal[jc][:, block(quarter)], ident_f[:], inv_sum[:, quarter : quarter + 1])
+                    nc.vector.tensor_scalar_mul(diagonal[:, block(quarter)], ident_f[:], inv_sum[:, quarter : quarter + 1])
 
-        def spread(jc):
+        def second_factor():
             spread_ps = psum_small.tile([LANES, BANK], F32, name="spread_ps", tag="spread")
-            nc.tensor.matmul(spread_ps[:], ones_f[:], diagonal[jc][:], start=True, stop=True)
-            nc.vector.tensor_tensor(factor[jc][:], spread_ps[:], deg[:, chunk(jc)], ALU.mult)
-
-        unplaced = []
-        factored = []
-
-        def place():
-            for first, width, cb, agg in unplaced:
-                if first // BANK in factored:
-                    piece = offsets[:, first // 16 : (first + width) // 16]
-                    scale = factor[first // BANK][:, first % BANK : first % BANK + width]
-                    nc.vector.tensor_tensor(window[cb][:].indirect(piece), agg[:], scale, ALU.mult)
-                    if first + width == N:
-                        nc.sync.dma_start(out[block(cb), :], window[cb][:])
-            still_waiting = [entry for entry in unplaced if entry[0] // BANK not in factored]
-            unplaced.clear()
-            unplaced.extend(still_waiting)
+            nc.tensor.matmul(spread_ps[:], ones_f[:], diagonal[:], start=True, stop=True)
+            nc.vector.tensor_tensor(factor[1][:], spread_ps[:], deg[:, chunk(1)], ALU.mult)
 
         passes = [(0, BANK, (0, 1)), (0, BANK, (2,)), (0, BANK, (3,))]
         passes.extend((BANK + half * HALF, HALF, (cb,)) for cb in range(CB) for half in range(BANK // HALF))
         for index, (first, width, together) in enumerate(passes):
             jc = first // BANK
             edges = slice(first % BANK, first % BANK + width)
-            rider = index // 2
             agg_ps = {cb: psum_long.tile([LANES, BANK], F32, name=f"agg_ps{cb}", tag="long") for cb in together}
             for nb in range(NB):
                 for cb in together:
@@ -208,14 +201,16 @@ def tile_whnnaggregator_b_kernel(
                     )
                     others += 1
                     feed_scalar(others)
-                if rider < JC and index % 2 == 0 and nb >= NB - QUARTERS:
-                    column_sum(rider, nb - (NB - QUARTERS))
-                if rider < JC and index % 2 == 1 and nb == min(NB, COVER * BANK // width) - 1:
-                    spread(rider)
-                    factored.append(rider)
-                    place()
+                if index == 0 and nb == NB - QUARTERS:
+                    first_factor()
+                if index == 2 and nb >= NB - QUARTERS:
+                    column_sum(nb - (NB - QUARTERS))
+                if index == 3 and nb == NB - 1:
+                    second_factor()
             for cb in together:
                 agg = held.tile([LANES, width], F32, name=f"agg{first}_{cb}")
                 nc.scalar.copy(agg[:], agg_ps[cb][:, 0:width])
-                unplaced.append((first, width, cb, agg))
-            place()
+                piece = offsets[:, first // 16 : (first + width) // 16]
+                nc.vector.tensor_tensor(window[cb][:].indirect(piece), agg[:], factor[jc][:, edges], ALU.mult)
+                if first + width == N:
+                    nc.sync.dma_start(out[block(cb), :], window[cb][:])

@@ -65,11 +65,13 @@ def tile_whnnaggregator_b_kernel(
         member = held.tile([LANES, NB, N], BF16, name="member")
         incidence_blocks = incidence.rearrange("(nb n) j -> n nb j", n=LANES)
         offsets = held.tile([LANES, N // 16], U16, name="offsets")
-        nc.sync.dma_start(member[:, :, chunk(0)], incidence_blocks[:, :, chunk(0)])
+        for g in range(NB // GROUP):
+            nc.sync.dma_start(member[:, group(g), chunk(0)], incidence_blocks[:, group(g), chunk(0)])
         deg = held.tile([LANES, N], F32, name="deg")
         nc.sync.dma_start(deg[:], inv_deg[0, :].partition_broadcast(LANES))
         nc.sync.dma_start(offsets[:], offs)
-        nc.sync.dma_start(member[:, :, chunk(1)], incidence_blocks[:, :, chunk(1)])
+        for g in range(NB // GROUP):
+            nc.sync.dma_start(member[:, group(g), chunk(1)], incidence_blocks[:, group(g), chunk(1)])
         window = [held.tile([LANES, S], F32, name=f"window{cb}") for cb in range(CB)]
         for cb in range(CB):
             nc.sync.dma_start(window[cb][:], base[block(cb), :])

@@ -68,10 +68,11 @@ def tile_whnnaggregator_b_kernel(
         for g in range(NB // GROUP):
             nc.sync.dma_start(member[:, group(g), chunk(0)], incidence_blocks[:, group(g), chunk(0)])
         deg = held.tile([LANES, N], F32, name="deg")
-        nc.sync.dma_start(deg[:], inv_deg[0, :].partition_broadcast(LANES))
+        nc.sync.dma_start(deg[:, chunk(0)], inv_deg[0, chunk(0)].partition_broadcast(LANES))
         nc.sync.dma_start(offsets[:], offs)
         for g in range(NB // GROUP):
             nc.sync.dma_start(member[:, group(g), chunk(1)], incidence_blocks[:, group(g), chunk(1)])
+        nc.sync.dma_start(deg[:, chunk(1)], inv_deg[0, chunk(1)].partition_broadcast(LANES))
         window = [held.tile([LANES, S], F32, name=f"window{cb}") for cb in range(CB)]
         for cb in range(CB):
             nc.sync.dma_start(window[cb][:], base[block(cb), :])

@@ -104,10 +104,25 @@ def tile_whnnaggregator_b_kernel(
         nc.vector.tensor_mul(k_shift[:], mean[:], k_scale[:])
         nc.vector.tensor_sub(k_shift[:], beta[:], k_shift[:])
 
+        untransposed = [(nb, cb) for nb in range(NB) for cb in range(CB)]
+        ft_ps = {}
+
+        def transpose_one():
+            if untransposed:
+                nb, cb = untransposed.pop(0)
+                first = nb - nb % PAIR
+                if (nb, cb) == (first, 0):
+                    ft_ps[first] = psum_long.tile([LANES, PAIR, CB, LANES], BF16, name="ft_ps", tag="long")
+                nc.tensor.transpose(ft_ps[first][:, nb - first, cb, :], feat[:, cb, block(nb)], ident_b[:])
+                if (nb, cb) == (first + PAIR - 1, CB - 1):
+                    copy = nc.scalar.copy if first < NB // 2 else nc.vector.tensor_copy
+                    copy(feat_t[:, first : first + PAIR, :, :], ft_ps[first][:])
+
         def keys_of(g):
             k_ps = psum_work.tile([LANES, BANK], F32, name="k_ps", tag="work")
             for cb in range(CB):
                 nc.tensor.matmul(k_ps[:], weights[:, cb, :], feat[:, cb, chunk(g)], start=(cb == 0), stop=(cb == CB - 1))
+                transpose_one()
             nc.vector.tensor_scalar(keys[:, chunk(g)], k_ps[:], k_scale[:], k_shift[:], ALU.mult, ALU.add)
 
         def keys_transposed(g):
@@ -116,19 +131,12 @@ def tile_whnnaggregator_b_kernel(
                 nc.tensor.transpose(kt_ps[:, i, :], keys[:, block(g * GROUP + i)], ident_b[:])
             nc.scalar.copy(keys_t[:, group(g), :], kt_ps[:])
 
-        def features_transposed(first, copy):
-            ft_ps = psum_long.tile([LANES, PAIR, CB, LANES], BF16, name="ft_ps", tag="long")
-            for i in range(PAIR):
-                for cb in range(CB):
-                    nc.tensor.transpose(ft_ps[:, i, cb, :], feat[:, cb, block(first + i)], ident_b[:])
-            copy(feat_t[:, first : first + PAIR, :, :], ft_ps[:])
-
         for g in range(NB // GROUP):
             keys_of(g)
-            if g > 0:
-                keys_transposed(g - 1)
-            features_transposed(g * GROUP, nc.scalar.copy)
-            features_transposed(g * GROUP + PAIR, nc.vector.tensor_copy)
+        for g in range(NB // GROUP - 1):
+            keys_transposed(g)
+        for i in range(len(untransposed) // 3):
+            transpose_one()
         keys_transposed(NB // GROUP - 1)
 
         def weights_of(jc, nb):
@@ -147,9 +155,10 @@ def tile_whnnaggregator_b_kernel(
             if others % 2 == 0 and 0 <= number < JC * NB:
                 weights_of(number // NB, number % NB)
 
-        proto_ps = psum_long.tile([LANES, BANK], F32, name="proto_ps", tag="long")
+        proto_ps = psum_small.tile([LANES, BANK], F32, name="proto_ps0", tag="spread")
         for nb in range(NB):
             nc.tensor.matmul(proto_ps[:], keys_t[:, nb, :], member[:, nb, chunk(0)], start=(nb == 0), stop=(nb == NB - 1))
+            transpose_one()
         for g in range(NB // GROUP):
             nc.scalar.activation(
                 squares[:, group(g), :], keys_t[:, group(g), :], ACT.Square, scale=math.sqrt(1.0 / TEMPERATURE)
@@ -158,9 +167,10 @@ def tile_whnnaggregator_b_kernel(
         nc.vector.tensor_tensor(proto[:, chunk(0)], proto_ps[:], deg[:, chunk(0)], ALU.mult)
 
         others = 0
-        proto_ps = psum_long.tile([LANES, BANK], F32, name="proto_ps", tag="long")
+        proto_ps = psum_small.tile([LANES, BANK], F32, name="proto_ps1", tag="column")
         for nb in range(NB):
             nc.tensor.matmul(proto_ps[:], keys_t[:, nb, :], member[:, nb, chunk(1)], start=(nb == 0), stop=(nb == NB - 1))
+            transpose_one()
             others += 1
             feed_scalar(others)
         nc.vector.tensor_tensor(proto[:, chunk(1)], proto_ps[:], deg[:, chunk(1)], ALU.mult)

@@ -20,7 +20,8 @@ NB = V // LANES
 JC = N // BANK
 QUARTERS = BANK // LANES
 GROUP = 4
-PAIR = 2
+OCTET = 8
+HALVES = NB // OCTET
 LEAD = 4
 HALF = BANK // 2
 
@@ -37,6 +38,10 @@ def group(i):
     return slice(i * GROUP, (i + 1) * GROUP)
 
 
+def octet(i):
+    return slice(i * OCTET, (i + 1) * OCTET)
+
+
 def tile_whnnaggregator_b_kernel(
     tc, vertex_feat, incidence, inv_deg, proj_w, bn_gamma, bn_beta, bn_mean, bn_var, base, offs, out
 ):
@@ -48,20 +53,23 @@ def tile_whnnaggregator_b_kernel(
         tc.psum_pool(name="psum_small", bufs=1) as psum_small,
     ):
         weights = held.tile([LANES, CB, P], BF16, name="weights")
-        nc.sync.dma_start(weights[:], proj_w.rearrange("(cb c) p -> c cb p", c=LANES))
-        feat = held.tile([LANES, CB, V], BF16, name="feat")
-        feat_blocks = vertex_feat.rearrange("(cb c) n -> c cb n", c=LANES)
+        weight_blocks = proj_w.rearrange("(c cb) p -> c cb p", cb=CB)
+        nc.sync.dma_start(weights[:, 0:1, :], weight_blocks[:, 0:1, :])
+        feat = [[held.tile([LANES, V // HALVES], BF16, name=f"feat{h}_{cb}") for cb in range(CB)] for h in range(HALVES)]
+        feat_blocks = vertex_feat.rearrange("(c cb) (h n) -> h cb c n", cb=CB, h=HALVES)
         var = held.tile([LANES, 1], F32, name="var")
         gamma = held.tile([LANES, 1], F32, name="gamma")
         mean = held.tile([LANES, 1], F32, name="mean")
         beta = held.tile([LANES, 1], F32, name="beta")
-        nc.scalar.dma_start(var[:], bn_var)
-        nc.scalar.dma_start(gamma[:], bn_gamma)
-        for g in range(NB // GROUP):
-            nc.sync.dma_start(feat[:, :, chunk(g)], feat_blocks[:, :, chunk(g)])
-            if g == 0:
-                nc.sync.dma_start(mean[:], bn_mean)
-                nc.sync.dma_start(beta[:], bn_beta)
+        nc.scalar.dma_start(feat[0][0][:, chunk(0)], feat_blocks[0, 0][:, chunk(0)])
+        nc.sync.dma_start(feat[0][0][:, chunk(1)], feat_blocks[0, 0][:, chunk(1)])
+        nc.scalar.dma_start(weights[:, 1:CB, :], weight_blocks[:, 1:CB, :])
+        for vector, source in ((var, bn_var), (gamma, bn_gamma), (mean, bn_mean), (beta, bn_beta)):
+            nc.scalar.dma_start(vector[:], source)
+        for piece in range(1, HALVES * CB):
+            queue = nc.scalar if piece % 2 == 0 else nc.sync
+            h, cb = divmod(piece, CB)
+            queue.dma_start(feat[h][cb][:], feat_blocks[h, cb])
         member = held.tile([LANES, NB, N], BF16, name="member")
         incidence_blocks = incidence.rearrange("(nb n) j -> n nb j", n=LANES)
         offsets = held.tile([LANES, N // 16], U16, name="offsets")
@@ -73,9 +81,11 @@ def tile_whnnaggregator_b_kernel(
         for g in range(NB // GROUP):
             nc.sync.dma_start(member[:, group(g), chunk(1)], incidence_blocks[:, group(g), chunk(1)])
         nc.sync.dma_start(deg[:, chunk(1)], inv_deg[0, chunk(1)].partition_broadcast(LANES))
+        base_blocks = base.rearrange("(c cb) s -> cb c s", cb=CB)
+        out_blocks = out.rearrange("(c cb) s -> cb c s", cb=CB)
         window = [held.tile([LANES, S], F32, name=f"window{cb}") for cb in range(CB)]
         for cb in range(CB):
-            nc.sync.dma_start(window[cb][:], base[block(cb), :])
+            nc.sync.dma_start(window[cb][:], base_blocks[cb])
 
         ident_f = held.tile([LANES, LANES], F32, name="ident_f")
         make_identity(nc, ident_f[:])
@@ -90,58 +100,86 @@ def tile_whnnaggregator_b_kernel(
         keys_t = held.tile([LANES, NB, P], BF16, name="keys_t")
         squares = held.tile([LANES, NB, P], F32, name="squares")
         neg_norm = held.tile([LANES, NB], F32, name="neg_norm")
-        feat_t = held.tile([LANES, NB, CB, LANES], BF16, name="feat_t")
+        feat_t = held.tile([LANES, CB, NB, LANES], BF16, name="feat_t")
         proto = held.tile([LANES, N], BF16, name="proto")
         soft = [held.tile([LANES, NB, BANK], BF16, name=f"soft{jc}") for jc in range(JC)]
         lane_sum = held.tile([LANES, BANK], F32, name="lane_sum")
         factor = [held.tile([LANES, BANK], F32, name=f"factor{jc}") for jc in range(JC)]
 
 
+        minus_half = held.tile([LANES, 1], F32, name="minus_half")
+        var_eps = held.tile([LANES, 1], F32, name="var_eps")
+        inv_std = held.tile([LANES, 1], F32, name="inv_std")
         k_scale = held.tile([LANES, 1], F32, name="k_scale")
+        mean_scaled = held.tile([LANES, 1], F32, name="mean_scaled")
         k_shift = held.tile([LANES, 1], F32, name="k_shift")
-        nc.scalar.activation(k_scale[:], var[:], ACT.Abs_reciprocal_sqrt, bias=BN_EPS)
-        nc.vector.tensor_mul(k_scale[:], k_scale[:], gamma[:])
-        nc.vector.tensor_mul(k_shift[:], mean[:], k_scale[:])
-        nc.vector.tensor_sub(k_shift[:], beta[:], k_shift[:])
+        nc.gpsimd.memset(minus_half[:], -0.5)
+        nc.gpsimd.tensor_scalar_add(var_eps[:], var[:], BN_EPS)
+        nc.gpsimd.tensor_tensor(inv_std[:], var_eps[:], minus_half[:], ALU.pow)
+        nc.gpsimd.tensor_tensor(k_scale[:], inv_std[:], gamma[:], ALU.mult)
+        nc.gpsimd.tensor_tensor(mean_scaled[:], mean[:], k_scale[:], ALU.mult)
+        nc.gpsimd.tensor_tensor(k_shift[:], beta[:], mean_scaled[:], ALU.subtract)
 
-        untransposed = [(nb, cb) for nb in range(NB) for cb in range(CB)]
-        ft_ps = {}
+        waiting = []
 
-        def transpose_one():
-            if untransposed:
-                nb, cb = untransposed.pop(0)
-                first = nb - nb % PAIR
-                if (nb, cb) == (first, 0):
-                    ft_ps[first] = psum_long.tile([LANES, PAIR, CB, LANES], BF16, name="ft_ps", tag="long")
-                nc.tensor.transpose(ft_ps[first][:, nb - first, cb, :], feat[:, cb, block(nb)], ident_b[:])
-                if (nb, cb) == (first + PAIR - 1, CB - 1):
-                    copy = nc.scalar.copy if first < NB // 2 else nc.vector.tensor_copy
-                    copy(feat_t[:, first : first + PAIR, :, :], ft_ps[first][:])
+        def transposes_of_feat(h, cb):
+            ft_ps = []
 
-        def keys_of(g):
-            k_ps = psum_work.tile([LANES, BANK], F32, name="k_ps", tag="work")
+            def one(i):
+                if i == 0:
+                    ft_ps.append(psum_long.tile([LANES, OCTET, LANES], BF16, name="ft_ps", tag="long"))
+                nc.tensor.transpose(ft_ps[0][:, i, :], feat[h][cb][:, block(i)], ident_b[:])
+                if i == OCTET - 1:
+                    nc.vector.tensor_copy(feat_t[:, cb, octet(h), :], ft_ps[0][:])
+
+            return [(one, i) for i in range(OCTET)]
+
+        def transposes_of_keys(g):
+            kt_ps = []
+
+            def one(i):
+                if i == 0:
+                    pool, tag = ((psum_small, "spread"), (psum_small, "column"), (psum_work, "work"), (psum_work, "work"))[g]
+                    kt_ps.append(pool.tile([LANES, GROUP, P], BF16, name=f"kt_ps{g}", tag=tag))
+                nc.tensor.transpose(kt_ps[0][:, i, :], keys[:, block(g * GROUP + i)], ident_b[:])
+                if i == GROUP - 1:
+                    nc.scalar.copy(keys_t[:, group(g), :], kt_ps[0][:])
+
+            return [(one, i) for i in range(GROUP)]
+
+        def norms(g):
+            nc.scalar.activation(
+                squares[:, group(g), :], keys_t[:, group(g), :], ACT.Square, scale=math.sqrt(1.0 / TEMPERATURE)
+            )
+            nc.vector.tensor_reduce(neg_norm[:, group(g)], squares[:, group(g), :], axis=AXIS.X, op=ALU.add, negate=True)
+
+        def transpose_some(count):
+            for one, i in waiting[:count]:
+                one(i)
+            waiting[:count] = []
+
+        for h in range(HALVES):
+            banks = [(psum_small, "spread"), (psum_small, "column")] if h == 0 else [(psum_work, "work")] * 2
+            k_ps = [pool.tile([LANES, BANK], F32, name=f"k_ps{h}_{i}", tag=tag) for i, (pool, tag) in enumerate(banks)]
             for cb in range(CB):
-                nc.tensor.matmul(k_ps[:], weights[:, cb, :], feat[:, cb, chunk(g)], start=(cb == 0), stop=(cb == CB - 1))
-                transpose_one()
-            nc.vector.tensor_scalar(keys[:, chunk(g)], k_ps[:], k_scale[:], k_shift[:], ALU.mult, ALU.add)
-
-        def keys_transposed(g):
-            kt_ps = psum_work.tile([LANES, GROUP, P], BF16, name="kt_ps", tag="work")
-            for i in range(GROUP):
-                nc.tensor.transpose(kt_ps[:, i, :], keys[:, block(g * GROUP + i)], ident_b[:])
-            nc.scalar.copy(keys_t[:, group(g), :], kt_ps[:])
-
-        for g in range(NB // GROUP):
-            keys_of(g)
-        for g in range(NB // GROUP - 1):
-            keys_transposed(g)
-        for i in range(len(untransposed) // 3):
-            transpose_one()
-        keys_transposed(NB // GROUP - 1)
+                waiting.extend(transposes_of_feat(h, cb))
+                for i in range(2):
+                    nc.tensor.matmul(k_ps[i][:], weights[:, cb, :], feat[h][cb][:, chunk(i)], start=(cb == 0), stop=(cb == CB - 1))
+                    if (h, cb, i) != (0, 0, 0):
+                        transpose_some(2)
+            nc.vector.tensor_scalar(keys[:, chunk(2 * h)], k_ps[0][:], k_scale[:], k_shift[:], ALU.mult, ALU.add)
+            nc.scalar.activation(keys[:, chunk(2 * h + 1)], k_ps[1][:], ACT.Identity, bias=k_shift[:], scale=k_scale[:])
+            if h == 0:
+                waiting[GROUP + 2 : GROUP + 2] = transposes_of_keys(0) + transposes_of_keys(1)
+        transpose_some(OCTET + 2)
+        norms(0)
+        norms(1)
+        waiting[:0] = transposes_of_keys(2) + transposes_of_keys(3)
 
         def weights_of(jc, nb):
             dot_ps = psum_work.tile([LANES, BANK], F32, name="dot_ps", tag="work")
             nc.tensor.matmul(dot_ps[:], keys[:, block(nb)], proto[:, chunk(jc)], start=True, stop=True)
+            transpose_some(1)
             nc.scalar.activation(
                 soft[jc][:, nb, :], dot_ps[:], ACT.Exp, bias=neg_norm[:, nb : nb + 1], scale=2.0 / TEMPERATURE
             )
@@ -158,19 +196,18 @@ def tile_whnnaggregator_b_kernel(
         proto_ps = psum_small.tile([LANES, BANK], F32, name="proto_ps0", tag="spread")
         for nb in range(NB):
             nc.tensor.matmul(proto_ps[:], keys_t[:, nb, :], member[:, nb, chunk(0)], start=(nb == 0), stop=(nb == NB - 1))
-            transpose_one()
-        for g in range(NB // GROUP):
-            nc.scalar.activation(
-                squares[:, group(g), :], keys_t[:, group(g), :], ACT.Square, scale=math.sqrt(1.0 / TEMPERATURE)
-            )
-            nc.vector.tensor_reduce(neg_norm[:, group(g)], squares[:, group(g), :], axis=AXIS.X, op=ALU.add, negate=True)
+            if nb > 0:
+                transpose_some(2 if nb <= GROUP else 1)
+            if nb == GROUP:
+                norms(2)
+                norms(3)
         nc.vector.tensor_tensor(proto[:, chunk(0)], proto_ps[:], deg[:, chunk(0)], ALU.mult)
 
         others = 0
         proto_ps = psum_small.tile([LANES, BANK], F32, name="proto_ps1", tag="column")
         for nb in range(NB):
             nc.tensor.matmul(proto_ps[:], keys_t[:, nb, :], member[:, nb, chunk(1)], start=(nb == 0), stop=(nb == NB - 1))
-            transpose_one()
+            transpose_some(1)
             others += 1
             feed_scalar(others)
         nc.vector.tensor_tensor(proto[:, chunk(1)], proto_ps[:], deg[:, chunk(1)], ALU.mult)
@@ -210,7 +247,7 @@ def tile_whnnaggregator_b_kernel(
             for nb in range(NB):
                 for cb in together:
                     nc.tensor.matmul(
-                        agg_ps[cb][:, 0:width], feat_t[:, nb, cb, :], soft[jc][:, nb, edges], start=(nb == 0), stop=(nb == NB - 1)
+                        agg_ps[cb][:, 0:width], feat_t[:, cb, nb, :], soft[jc][:, nb, edges], start=(nb == 0), stop=(nb == NB - 1)
                     )
                     others += 1
                     feed_scalar(others)
@@ -226,4 +263,4 @@ def tile_whnnaggregator_b_kernel(
                 piece = offsets[:, first // 16 : (first + width) // 16]
                 nc.vector.tensor_tensor(window[cb][:].indirect(piece), agg[:], factor[jc][:, edges], ALU.mult)
                 if first + width == N:
-                    nc.sync.dma_start(out[block(cb), :], window[cb][:])
+                    nc.sync.dma_start(out_blocks[cb], window[cb][:])

@@ -52,24 +52,44 @@ def tile_whnnaggregator_b_kernel(
         tc.psum_pool(name="psum_long", bufs=3) as psum_long,
         tc.psum_pool(name="psum_small", bufs=1) as psum_small,
     ):
+        ident_f = held.tile([LANES, LANES], F32, name="ident_f")
+        make_identity(nc, ident_f[:])
+        ident_b = held.tile([LANES, LANES], BF16, name="ident_b")
+        nc.vector.tensor_copy(ident_b[:], ident_f[:])
+        ones_f = held.tile([LANES, LANES], F32, name="ones_f")
+        nc.vector.memset(ones_f[:], 1.0)
+        one_column = held.tile([LANES, 1], BF16, name="one_column")
+
         weights = held.tile([LANES, CB, P], BF16, name="weights")
         weight_blocks = proj_w.rearrange("(c cb) p -> c cb p", cb=CB)
-        nc.sync.dma_start(weights[:, 0:1, :], weight_blocks[:, 0:1, :])
-        feat = [[held.tile([LANES, V // HALVES], BF16, name=f"feat{h}_{cb}") for cb in range(CB)] for h in range(HALVES)]
-        feat_blocks = vertex_feat.rearrange("(c cb) (h n) -> h cb c n", cb=CB, h=HALVES)
+        feat = [held.tile([LANES, CB, V // HALVES], BF16, name=f"feat{h}") for h in range(HALVES)]
+        feat_halves = vertex_feat.rearrange("(c cb) (h n) -> h c cb n", cb=CB, h=HALVES)
         var = held.tile([LANES, 1], F32, name="var")
         gamma = held.tile([LANES, 1], F32, name="gamma")
         mean = held.tile([LANES, 1], F32, name="mean")
         beta = held.tile([LANES, 1], F32, name="beta")
-        nc.scalar.dma_start(feat[0][0][:, chunk(0)], feat_blocks[0, 0][:, chunk(0)])
-        nc.sync.dma_start(feat[0][0][:, chunk(1)], feat_blocks[0, 0][:, chunk(1)])
-        nc.scalar.dma_start(weights[:, 1:CB, :], weight_blocks[:, 1:CB, :])
-        for vector, source in ((var, bn_var), (gamma, bn_gamma), (mean, bn_mean), (beta, bn_beta)):
-            nc.scalar.dma_start(vector[:], source)
-        for piece in range(1, HALVES * CB):
-            queue = nc.scalar if piece % 2 == 0 else nc.sync
-            h, cb = divmod(piece, CB)
-            queue.dma_start(feat[h][cb][:], feat_blocks[h, cb])
+
+        def load_weights(queue, blocks):
+            queue.dma_start(weights[:, blocks, :], weight_blocks[:, blocks, :])
+
+        def load_feat(queue, h, cb, columns=slice(0, V // HALVES)):
+            queue.dma_start(feat[h][:, cb, columns], feat_halves[h][:, cb, columns])
+
+        load_weights(nc.sync, slice(0, 1))
+        load_feat(nc.scalar, 0, 0, chunk(0))
+        load_feat(nc.sync, 0, 0, chunk(1))
+        load_weights(nc.scalar, slice(1, CB))
+        nc.scalar.dma_start(var[:], bn_var)
+        load_feat(nc.sync, 0, 1)
+        load_feat(nc.scalar, 0, 2)
+        nc.scalar.activation(one_column[:], ident_f[:, 0:1], ACT.Exp, scale=0.0)
+        load_feat(nc.sync, 0, 3)
+        load_feat(nc.sync, 1, 0)
+        nc.scalar.dma_start(gamma[:], bn_gamma)
+        nc.scalar.dma_start(mean[:], bn_mean)
+        nc.scalar.dma_start(beta[:], bn_beta)
+        for cb in range(1, CB):
+            load_feat(nc.sync, 1, cb)
         member = held.tile([LANES, NB, N], BF16, name="member")
         incidence_blocks = incidence.rearrange("(nb n) j -> n nb j", n=LANES)
         offsets = held.tile([LANES, N // 16], U16, name="offsets")
@@ -86,15 +106,6 @@ def tile_whnnaggregator_b_kernel(
         window = [held.tile([LANES, S], F32, name=f"window{cb}") for cb in range(CB)]
         for cb in range(CB):
             nc.sync.dma_start(window[cb][:], base_blocks[cb])
-
-        ident_f = held.tile([LANES, LANES], F32, name="ident_f")
-        make_identity(nc, ident_f[:])
-        ident_b = held.tile([LANES, LANES], BF16, name="ident_b")
-        nc.vector.tensor_copy(ident_b[:], ident_f[:])
-        ones_b = held.tile([LANES, LANES], BF16, name="ones_b")
-        nc.vector.memset(ones_b[:], 1.0)
-        ones_f = held.tile([LANES, LANES], F32, name="ones_f")
-        nc.vector.memset(ones_f[:], 1.0)
 
         keys = held.tile([LANES, V], BF16, name="keys")
         keys_t = held.tile([LANES, NB, P], BF16, name="keys_t")
@@ -120,32 +131,29 @@ def tile_whnnaggregator_b_kernel(
         nc.gpsimd.tensor_tensor(mean_scaled[:], mean[:], k_scale[:], ALU.mult)
         nc.gpsimd.tensor_tensor(k_shift[:], beta[:], mean_scaled[:], ALU.subtract)
 
-        waiting = []
+        feat_blocks = [(h, cb, i) for h in range(HALVES) for cb in range(CB) for i in range(OCTET)]
+        key_blocks = [(g, i) for g in range(NB // GROUP) for i in range(GROUP)]
+        ft_ps, kt_ps = {}, {}
 
-        def transposes_of_feat(h, cb):
-            ft_ps = []
-
-            def one(i):
+        def transpose_feat(count):
+            for h, cb, i in feat_blocks[:count]:
                 if i == 0:
-                    ft_ps.append(psum_long.tile([LANES, OCTET, LANES], BF16, name="ft_ps", tag="long"))
-                nc.tensor.transpose(ft_ps[0][:, i, :], feat[h][cb][:, block(i)], ident_b[:])
+                    pool, tag = (psum_small, "spread") if (h, cb) == (HALVES - 1, CB - 1) else (psum_long, "long")
+                    ft_ps[h, cb] = pool.tile([LANES, OCTET, LANES], BF16, name=f"ft_ps{h}_{cb}", tag=tag)
+                nc.tensor.transpose(ft_ps[h, cb][:, i, :], feat[h][:, cb, block(i)], ident_b[:])
                 if i == OCTET - 1:
-                    nc.vector.tensor_copy(feat_t[:, cb, octet(h), :], ft_ps[0][:])
+                    nc.vector.tensor_copy(feat_t[:, cb, octet(h), :], ft_ps[h, cb][:])
+            feat_blocks[:count] = []
 
-            return [(one, i) for i in range(OCTET)]
-
-        def transposes_of_keys(g):
-            kt_ps = []
-
-            def one(i):
+        def transpose_keys(count):
+            for g, i in key_blocks[:count]:
                 if i == 0:
-                    pool, tag = ((psum_small, "spread"), (psum_small, "column"), (psum_work, "work"), (psum_work, "work"))[g]
-                    kt_ps.append(pool.tile([LANES, GROUP, P], BF16, name=f"kt_ps{g}", tag=tag))
-                nc.tensor.transpose(kt_ps[0][:, i, :], keys[:, block(g * GROUP + i)], ident_b[:])
+                    pool, tag = (psum_work, "work") if g > 1 else (psum_small, ("spread", "column")[g])
+                    kt_ps[g] = pool.tile([LANES, GROUP, P], BF16, name=f"kt_ps{g}", tag=tag)
+                nc.tensor.transpose(kt_ps[g][:, i, :], keys[:, block(g * GROUP + i)], ident_b[:])
                 if i == GROUP - 1:
-                    nc.scalar.copy(keys_t[:, group(g), :], kt_ps[0][:])
-
-            return [(one, i) for i in range(GROUP)]
+                    nc.scalar.copy(keys_t[:, group(g), :], kt_ps[g][:])
+            key_blocks[:count] = []
 
         def norms(g):
             nc.scalar.activation(
@@ -153,33 +161,25 @@ def tile_whnnaggregator_b_kernel(
             )
             nc.vector.tensor_reduce(neg_norm[:, group(g)], squares[:, group(g), :], axis=AXIS.X, op=ALU.add, negate=True)
 
-        def transpose_some(count):
-            for one, i in waiting[:count]:
-                one(i)
-            waiting[:count] = []
-
         for h in range(HALVES):
             banks = [(psum_small, "spread"), (psum_small, "column")] if h == 0 else [(psum_work, "work")] * 2
             k_ps = [pool.tile([LANES, BANK], F32, name=f"k_ps{h}_{i}", tag=tag) for i, (pool, tag) in enumerate(banks)]
             for cb in range(CB):
-                waiting.extend(transposes_of_feat(h, cb))
                 for i in range(2):
-                    nc.tensor.matmul(k_ps[i][:], weights[:, cb, :], feat[h][cb][:, chunk(i)], start=(cb == 0), stop=(cb == CB - 1))
-                    if (h, cb, i) != (0, 0, 0):
-                        transpose_some(2)
+                    nc.tensor.matmul(k_ps[i][:], weights[:, cb, :], feat[h][:, cb, chunk(i)], start=(cb == 0), stop=(cb == CB - 1))
+                    if h == 1 and 3 <= 2 * cb + i < 7:
+                        transpose_keys(2)
+                    elif (h, cb, i) != (0, 0, 0):
+                        transpose_feat(2)
             nc.vector.tensor_scalar(keys[:, chunk(2 * h)], k_ps[0][:], k_scale[:], k_shift[:], ALU.mult, ALU.add)
             nc.scalar.activation(keys[:, chunk(2 * h + 1)], k_ps[1][:], ACT.Identity, bias=k_shift[:], scale=k_scale[:])
-            if h == 0:
-                waiting[GROUP + 2 : GROUP + 2] = transposes_of_keys(0) + transposes_of_keys(1)
-        transpose_some(OCTET + 2)
         norms(0)
         norms(1)
-        waiting[:0] = transposes_of_keys(2) + transposes_of_keys(3)
 
         def weights_of(jc, nb):
             dot_ps = psum_work.tile([LANES, BANK], F32, name="dot_ps", tag="work")
             nc.tensor.matmul(dot_ps[:], keys[:, block(nb)], proto[:, chunk(jc)], start=True, stop=True)
-            transpose_some(1)
+            transpose_feat(1)
             nc.scalar.activation(
                 soft[jc][:, nb, :], dot_ps[:], ACT.Exp, bias=neg_norm[:, nb : nb + 1], scale=2.0 / TEMPERATURE
             )
@@ -196,9 +196,11 @@ def tile_whnnaggregator_b_kernel(
         proto_ps = psum_small.tile([LANES, BANK], F32, name="proto_ps0", tag="spread")
         for nb in range(NB):
             nc.tensor.matmul(proto_ps[:], keys_t[:, nb, :], member[:, nb, chunk(0)], start=(nb == 0), stop=(nb == NB - 1))
-            if nb > 0:
-                transpose_some(2 if nb <= GROUP else 1)
-            if nb == GROUP:
+            if 2 <= nb < 6:
+                transpose_keys(2)
+            else:
+                transpose_feat(1)
+            if nb == 5:
                 norms(2)
                 norms(3)
         nc.vector.tensor_tensor(proto[:, chunk(0)], proto_ps[:], deg[:, chunk(0)], ALU.mult)
@@ -207,7 +209,7 @@ def tile_whnnaggregator_b_kernel(
         proto_ps = psum_small.tile([LANES, BANK], F32, name="proto_ps1", tag="column")
         for nb in range(NB):
             nc.tensor.matmul(proto_ps[:], keys_t[:, nb, :], member[:, nb, chunk(1)], start=(nb == 0), stop=(nb == NB - 1))
-            transpose_some(1)
+            transpose_feat(1)
             others += 1
             feed_scalar(others)
         nc.vector.tensor_tensor(proto[:, chunk(1)], proto_ps[:], deg[:, chunk(1)], ALU.mult)
@@ -225,7 +227,7 @@ def tile_whnnaggregator_b_kernel(
         def column_sum(q):
             for nb in range(NB):
                 nc.tensor.matmul(
-                    sum_ps[:, q : q + 1], soft[1][:, nb, block(q)], ones_b[:, 0:1], start=(nb == 0), stop=(nb == NB - 1)
+                    sum_ps[:, q : q + 1], soft[1][:, nb, block(q)], one_column[:], start=(nb == 0), stop=(nb == NB - 1)
                 )
             if q == QUARTERS - 1:
                 inv_sum = held.tile([LANES, QUARTERS], F32, name="inv_sum")
@@ -251,7 +253,7 @@ def tile_whnnaggregator_b_kernel(
                     )
                     others += 1
                     feed_scalar(others)
-                if index == 0 and nb == NB - QUARTERS:
+                if index == 0 and nb == NB - 2:
                     first_factor()
                 if index == 2 and nb >= NB - QUARTERS:
                     column_sum(nb - (NB - QUARTERS))

@@ -59,6 +59,7 @@ def tile_whnnaggregator_b_kernel(
         ones_f = held.tile([LANES, LANES], F32, name="ones_f")
         nc.vector.memset(ones_f[:], 1.0)
         one_column = held.tile([LANES, 1], BF16, name="one_column")
+        nc.vector.memset(one_column[:], 1.0)
 
         weights = held.tile([LANES, CB, P], BF16, name="weights")
         weight_blocks = proj_w.rearrange("(c cb) p -> c cb p", cb=CB)
@@ -82,7 +83,6 @@ def tile_whnnaggregator_b_kernel(
         nc.scalar.dma_start(var[:], bn_var)
         load_feat(nc.sync, 0, 1)
         load_feat(nc.scalar, 0, 2)
-        nc.scalar.activation(one_column[:], ident_f[:, 0:1], ACT.Exp, scale=0.0)
         load_feat(nc.sync, 0, 3)
         load_feat(nc.sync, 1, 0)
         nc.scalar.dma_start(gamma[:], bn_gamma)
@@ -118,18 +118,12 @@ def tile_whnnaggregator_b_kernel(
         factor = [held.tile([LANES, BANK], F32, name=f"factor{jc}") for jc in range(JC)]
 
 
-        minus_half = held.tile([LANES, 1], F32, name="minus_half")
-        var_eps = held.tile([LANES, 1], F32, name="var_eps")
-        inv_std = held.tile([LANES, 1], F32, name="inv_std")
         k_scale = held.tile([LANES, 1], F32, name="k_scale")
-        mean_scaled = held.tile([LANES, 1], F32, name="mean_scaled")
         k_shift = held.tile([LANES, 1], F32, name="k_shift")
-        nc.gpsimd.memset(minus_half[:], -0.5)
-        nc.gpsimd.tensor_scalar_add(var_eps[:], var[:], BN_EPS)
-        nc.gpsimd.tensor_tensor(inv_std[:], var_eps[:], minus_half[:], ALU.pow)
-        nc.gpsimd.tensor_tensor(k_scale[:], inv_std[:], gamma[:], ALU.mult)
-        nc.gpsimd.tensor_tensor(mean_scaled[:], mean[:], k_scale[:], ALU.mult)
-        nc.gpsimd.tensor_tensor(k_shift[:], beta[:], mean_scaled[:], ALU.subtract)
+        nc.scalar.activation(k_scale[:], var[:], ACT.Abs_reciprocal_sqrt, bias=BN_EPS)
+        nc.vector.tensor_mul(k_scale[:], k_scale[:], gamma[:])
+        nc.vector.tensor_mul(k_shift[:], mean[:], k_scale[:])
+        nc.vector.tensor_sub(k_shift[:], beta[:], k_shift[:])
 
         feat_blocks = [(h, cb, i) for h in range(HALVES) for cb in range(CB) for i in range(OCTET)]
         key_blocks = [(g, i) for g in range(NB // GROUP) for i in range(GROUP)]

@@ -58,6 +58,8 @@ def tile_whnnaggregator_b_kernel(
         nc.vector.tensor_copy(ident_b[:], ident_f[:])
         ones_f = held.tile([LANES, LANES], F32, name="ones_f")
         nc.vector.memset(ones_f[:], 1.0)
+        deg_row = held.tile([LANES, BANK], F32, name="deg_row")
+        nc.gpsimd.memset(deg_row[:], 0.0)
         one_column = held.tile([LANES, 1], BF16, name="one_column")
         nc.vector.memset(one_column[:], 1.0)
 
@@ -88,15 +90,16 @@ def tile_whnnaggregator_b_kernel(
         nc.scalar.dma_start(gamma[:], bn_gamma)
         nc.scalar.dma_start(mean[:], bn_mean)
         nc.scalar.dma_start(beta[:], bn_beta)
-        for cb in range(1, CB):
+        for cb in range(1, CB - 1):
             load_feat(nc.sync, 1, cb)
+        nc.sync.dma_start(deg_row[0:1, :], inv_deg[0:1, chunk(0)])
+        load_feat(nc.sync, 1, CB - 1)
         member = held.tile([LANES, NB, N], BF16, name="member")
         incidence_blocks = incidence.rearrange("(nb n) j -> n nb j", n=LANES)
         offsets = held.tile([LANES, N // 16], U16, name="offsets")
         for g in range(NB // GROUP):
             nc.sync.dma_start(member[:, group(g), chunk(0)], incidence_blocks[:, group(g), chunk(0)])
         deg = held.tile([LANES, N], F32, name="deg")
-        nc.sync.dma_start(deg[:, chunk(0)], inv_deg[0, chunk(0)].partition_broadcast(LANES))
         nc.sync.dma_start(offsets[:], offs)
         for g in range(NB // GROUP):
             nc.sync.dma_start(member[:, group(g), chunk(1)], incidence_blocks[:, group(g), chunk(1)])
@@ -132,7 +135,7 @@ def tile_whnnaggregator_b_kernel(
         def transpose_feat(count):
             for h, cb, i in feat_blocks[:count]:
                 if i == 0:
-                    pool, tag = (psum_small, "spread") if (h, cb) == (HALVES - 1, CB - 1) else (psum_long, "long")
+                    pool, tag = (psum_small, "spread") if (h, cb) == (HALVES - 1, CB - 2) else (psum_long, "long")
                     ft_ps[h, cb] = pool.tile([LANES, OCTET, LANES], BF16, name=f"ft_ps{h}_{cb}", tag=tag)
                 nc.tensor.transpose(ft_ps[h, cb][:, i, :], feat[h][:, cb, block(i)], ident_b[:])
                 if i == OCTET - 1:
@@ -167,6 +170,9 @@ def tile_whnnaggregator_b_kernel(
                         transpose_feat(2)
             nc.vector.tensor_scalar(keys[:, chunk(2 * h)], k_ps[0][:], k_scale[:], k_shift[:], ALU.mult, ALU.add)
             nc.scalar.activation(keys[:, chunk(2 * h + 1)], k_ps[1][:], ACT.Identity, bias=k_shift[:], scale=k_scale[:])
+        deg_ps = psum_work.tile([LANES, BANK], F32, name="deg_ps", tag="work")
+        nc.tensor.matmul(deg_ps[:], ones_f[:], deg_row[:], start=True, stop=True)
+        nc.scalar.copy(deg[:, chunk(0)], deg_ps[:])
         norms(0)
         norms(1)
 
@@ -201,12 +207,17 @@ def tile_whnnaggregator_b_kernel(
 
         others = 0
         proto_ps = psum_small.tile([LANES, BANK], F32, name="proto_ps1", tag="column")
-        for nb in range(NB):
+
+        def second_prototypes(nb):
             nc.tensor.matmul(proto_ps[:], keys_t[:, nb, :], member[:, nb, chunk(1)], start=(nb == 0), stop=(nb == NB - 1))
             transpose_feat(1)
+            if nb == NB - 1:
+                nc.vector.tensor_tensor(proto[:, chunk(1)], proto_ps[:], deg[:, chunk(1)], ALU.mult)
+
+        for nb in range(NB // 2):
+            second_prototypes(nb)
             others += 1
             feed_scalar(others)
-        nc.vector.tensor_tensor(proto[:, chunk(1)], proto_ps[:], deg[:, chunk(1)], ALU.mult)
 
 
         def first_factor():
@@ -247,6 +258,11 @@ def tile_whnnaggregator_b_kernel(
                     )
                     others += 1
                     feed_scalar(others)
+                if index == 0 and nb < NB // 4:
+                    for half in range(2):
+                        second_prototypes(NB // 2 + 2 * nb + half)
+                        others += 1
+                        feed_scalar(others)
                 if index == 0 and nb == NB - 2:
                     first_factor()
                 if index == 2 and nb >= NB - QUARTERS:

@@ -34,6 +34,10 @@ def chunk(i):
     return slice(i * BANK, (i + 1) * BANK)
 
 
+def vertices(i):
+    return slice(i // GROUP * BANK + i % GROUP, (i // GROUP + 1) * BANK, GROUP)
+
+
 def group(i):
     return slice(i * GROUP, (i + 1) * GROUP)
 
@@ -95,14 +99,12 @@ def tile_whnnaggregator_b_kernel(
         nc.sync.dma_start(deg_row[0:1, :], inv_deg[0:1, chunk(0)])
         load_feat(nc.sync, 1, CB - 1)
         member = held.tile([LANES, NB, N], BF16, name="member")
-        incidence_blocks = incidence.rearrange("(nb n) j -> n nb j", n=LANES)
+        incidence_groups = incidence.rearrange("(a n b) j -> a n b j", n=LANES, b=GROUP)
         offsets = held.tile([LANES, N // 16], U16, name="offsets")
-        for g in range(NB // GROUP):
-            nc.sync.dma_start(member[:, group(g), chunk(0)], incidence_blocks[:, group(g), chunk(0)])
+        for a in range(NB // GROUP):
+            nc.sync.dma_start(member[:, group(a), :], incidence_groups[a])
         deg = held.tile([LANES, N], F32, name="deg")
         nc.sync.dma_start(offsets[:], offs)
-        for g in range(NB // GROUP):
-            nc.sync.dma_start(member[:, group(g), chunk(1)], incidence_blocks[:, group(g), chunk(1)])
         nc.sync.dma_start(deg[:, chunk(1)], inv_deg[0, chunk(1)].partition_broadcast(LANES))
         base_blocks = base.rearrange("(c cb) s -> cb c s", cb=CB)
         out_blocks = out.rearrange("(c cb) s -> cb c s", cb=CB)
@@ -117,7 +119,8 @@ def tile_whnnaggregator_b_kernel(
         feat_t = held.tile([LANES, CB, NB, LANES], BF16, name="feat_t")
         proto = held.tile([LANES, N], BF16, name="proto")
         soft = [held.tile([LANES, NB, BANK], BF16, name=f"soft{jc}") for jc in range(JC)]
-        lane_sum = held.tile([LANES, BANK], F32, name="lane_sum")
+        lane_sum = [held.tile([LANES, BANK], F32, name=f"lane_sum{i}") for i in range(2)]
+        lane_total = held.tile([LANES, BANK], F32, name="lane_total")
         factor = [held.tile([LANES, BANK], F32, name=f"factor{jc}") for jc in range(JC)]
 
 
@@ -137,7 +140,7 @@ def tile_whnnaggregator_b_kernel(
                 if i == 0:
                     pool, tag = (psum_small, "spread") if (h, cb) == (HALVES - 1, CB - 2) else (psum_long, "long")
                     ft_ps[h, cb] = pool.tile([LANES, OCTET, LANES], BF16, name=f"ft_ps{h}_{cb}", tag=tag)
-                nc.tensor.transpose(ft_ps[h, cb][:, i, :], feat[h][:, cb, block(i)], ident_b[:])
+                nc.tensor.transpose(ft_ps[h, cb][:, i, :], feat[h][:, cb, vertices(i)], ident_b[:])
                 if i == OCTET - 1:
                     nc.vector.tensor_copy(feat_t[:, cb, octet(h), :], ft_ps[h, cb][:])
             feat_blocks[:count] = []
@@ -168,8 +171,10 @@ def tile_whnnaggregator_b_kernel(
                         transpose_keys(2)
                     elif (h, cb, i) != (0, 0, 0):
                         transpose_feat(2)
-            nc.vector.tensor_scalar(keys[:, chunk(2 * h)], k_ps[0][:], k_scale[:], k_shift[:], ALU.mult, ALU.add)
-            nc.scalar.activation(keys[:, chunk(2 * h + 1)], k_ps[1][:], ACT.Identity, bias=k_shift[:], scale=k_scale[:])
+            source = [k_ps[i][:].rearrange("p (n b) -> p b n", b=GROUP) for i in range(2)]
+            blocks = [keys[:, chunk(2 * h + i)].rearrange("p (b n) -> p b n", b=GROUP) for i in range(2)]
+            nc.vector.tensor_scalar(blocks[0], source[0], k_scale[:], k_shift[:], ALU.mult, ALU.add)
+            nc.scalar.activation(blocks[1], source[1], ACT.Identity, bias=k_shift[:], scale=k_scale[:])
         deg_ps = psum_work.tile([LANES, BANK], F32, name="deg_ps", tag="work")
         nc.tensor.matmul(deg_ps[:], ones_f[:], deg_row[:], start=True, stop=True)
         nc.scalar.copy(deg[:, chunk(0)], deg_ps[:])
@@ -183,46 +188,49 @@ def tile_whnnaggregator_b_kernel(
             nc.scalar.activation(
                 soft[jc][:, nb, :], dot_ps[:], ACT.Exp, bias=neg_norm[:, nb : nb + 1], scale=2.0 / TEMPERATURE
             )
-            if jc == 0 and nb == 1:
-                nc.vector.tensor_tensor(lane_sum[:], soft[0][:, 0, :], soft[0][:, 1, :], ALU.add)
-            if jc == 0 and nb > 1:
-                nc.vector.tensor_tensor(lane_sum[:], lane_sum[:], soft[0][:, nb, :], ALU.add)
+            if jc == 0 and nb in (2, 3):
+                nc.vector.tensor_tensor(lane_sum[nb % 2][:], soft[0][:, nb - 2, :], soft[0][:, nb, :], ALU.add)
+            if jc == 0 and nb > 3:
+                nc.vector.tensor_tensor(lane_sum[nb % 2][:], lane_sum[nb % 2][:], soft[0][:, nb, :], ALU.add)
+            if (jc, nb) == (0, NB - 1):
+                nc.vector.tensor_tensor(lane_total[:], lane_sum[0][:], lane_sum[1][:], ALU.add)
+
+        waiting_weights = [(jc, nb) for jc in range(JC) for nb in range(NB)]
 
         def feed_scalar(others):
-            number = (others - LEAD) // 2
-            if others % 2 == 0 and 0 <= number < JC * NB:
-                weights_of(number // NB, number % NB)
+            due = (others - LEAD) * 3 // 5 + 1
+            while waiting_weights and JC * NB - len(waiting_weights) < due:
+                weights_of(*waiting_weights.pop(0))
 
-        proto_ps = psum_small.tile([LANES, BANK], F32, name="proto_ps0", tag="spread")
-        for nb in range(NB):
-            nc.tensor.matmul(proto_ps[:], keys_t[:, nb, :], member[:, nb, chunk(0)], start=(nb == 0), stop=(nb == NB - 1))
-            if 2 <= nb < 6:
+        proto_ps = [psum_small.tile([LANES, BANK], F32, name=f"proto_ps{jc}", tag=tag) for jc, tag in enumerate(("spread", "column"))]
+
+        def prototypes(jc, nb):
+            nc.tensor.matmul(proto_ps[jc][:], keys_t[:, nb, :], member[:, nb, chunk(jc)], start=(nb == 0), stop=(nb == NB - 1))
+            if jc == 0 and 2 <= nb < 6:
                 transpose_keys(2)
             else:
                 transpose_feat(1)
+            if nb == NB - 1:
+                nc.vector.tensor_tensor(proto[:, chunk(jc)], proto_ps[jc][:], deg[:, chunk(jc)], ALU.mult)
+
+        for nb in range(NB):
+            prototypes(0, nb)
             if nb == 5:
                 norms(2)
                 norms(3)
-        nc.vector.tensor_tensor(proto[:, chunk(0)], proto_ps[:], deg[:, chunk(0)], ALU.mult)
-
+            if nb in (2 * GROUP - 1, 3 * GROUP - 1):
+                for early in range(nb + 1 - 2 * GROUP, nb + 1 - GROUP):
+                    prototypes(1, early)
         others = 0
-        proto_ps = psum_small.tile([LANES, BANK], F32, name="proto_ps1", tag="column")
-
-        def second_prototypes(nb):
-            nc.tensor.matmul(proto_ps[:], keys_t[:, nb, :], member[:, nb, chunk(1)], start=(nb == 0), stop=(nb == NB - 1))
-            transpose_feat(1)
-            if nb == NB - 1:
-                nc.vector.tensor_tensor(proto[:, chunk(1)], proto_ps[:], deg[:, chunk(1)], ALU.mult)
-
-        for nb in range(NB // 2):
-            second_prototypes(nb)
+        for nb in range(NB // 2, NB):
+            prototypes(1, nb)
             others += 1
             feed_scalar(others)
 
 
         def first_factor():
             total_ps = psum_small.tile([LANES, BANK], F32, name="total_ps", tag="spread")
-            nc.tensor.matmul(total_ps[:], ones_f[:], lane_sum[:], start=True, stop=True)
+            nc.tensor.matmul(total_ps[:], ones_f[:], lane_total[:], start=True, stop=True)
             nc.vector.reciprocal(factor[0][:], total_ps[:])
             nc.vector.tensor_tensor(factor[0][:], factor[0][:], deg[:, chunk(0)], ALU.mult)
 
@@ -258,12 +266,7 @@ def tile_whnnaggregator_b_kernel(
                     )
                     others += 1
                     feed_scalar(others)
-                if index == 0 and nb < NB // 4:
-                    for half in range(2):
-                        second_prototypes(NB // 2 + 2 * nb + half)
-                        others += 1
-                        feed_scalar(others)
-                if index == 0 and nb == NB - 2:
+                if index == 0 and nb == NB - 3:
                     first_factor()
                 if index == 2 and nb >= NB - QUARTERS:
                     column_sum(nb - (NB - QUARTERS))

@@ -86,23 +86,28 @@ def tile_whnnaggregator_b_kernel(
         load_feat(nc.scalar, 0, 0, chunk(0))
         load_feat(nc.sync, 0, 0, chunk(1))
         load_weights(nc.scalar, slice(1, CB))
+        nc.sync.dma_start(deg_row[0:1, :], inv_deg[0:1, chunk(0)])
         nc.scalar.dma_start(var[:], bn_var)
-        load_feat(nc.sync, 0, 1)
-        load_feat(nc.scalar, 0, 2)
-        load_feat(nc.sync, 0, 3)
+        for cb in range(1, CB):
+            load_feat(nc.sync, 0, cb)
         load_feat(nc.sync, 1, 0)
         nc.scalar.dma_start(gamma[:], bn_gamma)
         nc.scalar.dma_start(mean[:], bn_mean)
         nc.scalar.dma_start(beta[:], bn_beta)
-        for cb in range(1, CB - 1):
+        for cb in range(1, CB):
             load_feat(nc.sync, 1, cb)
-        nc.sync.dma_start(deg_row[0:1, :], inv_deg[0:1, chunk(0)])
-        load_feat(nc.sync, 1, CB - 1)
         member = held.tile([LANES, NB, N], BF16, name="member")
         incidence_groups = incidence.rearrange("(a n b) j -> a n b j", n=LANES, b=GROUP)
         offsets = held.tile([LANES, N // 16], U16, name="offsets")
-        for a in range(NB // GROUP):
-            nc.sync.dma_start(member[:, group(a), :], incidence_groups[a])
+        def load_member(a, rows=slice(0, GROUP), edges=slice(0, N)):
+            nc.sync.dma_start(member[:, group(a), :][:, rows, edges], incidence_groups[a][:, rows, edges])
+
+        load_member(0, rows=slice(0, GROUP // 2))
+        load_member(0, rows=slice(GROUP // 2, GROUP))
+        load_member(1)
+        load_member(2)
+        load_member(3, edges=chunk(0))
+        load_member(3, edges=chunk(1))
         deg = held.tile([LANES, N], F32, name="deg")
         nc.sync.dma_start(offsets[:], offs)
         nc.sync.dma_start(deg[:, chunk(1)], inv_deg[0, chunk(1)].partition_broadcast(LANES))
@@ -161,6 +166,11 @@ def tile_whnnaggregator_b_kernel(
             )
             nc.vector.tensor_reduce(neg_norm[:, group(g)], squares[:, group(g), :], axis=AXIS.X, op=ALU.add, negate=True)
 
+        def spread_degrees():
+            deg_ps = psum_work.tile([LANES, BANK], F32, name="deg_ps", tag="work")
+            nc.tensor.matmul(deg_ps[:], ones_f[:], deg_row[:], start=True, stop=True)
+            nc.scalar.copy(deg[:, chunk(0)], deg_ps[:])
+
         for h in range(HALVES):
             banks = [(psum_small, "spread"), (psum_small, "column")] if h == 0 else [(psum_work, "work")] * 2
             k_ps = [pool.tile([LANES, BANK], F32, name=f"k_ps{h}_{i}", tag=tag) for i, (pool, tag) in enumerate(banks)]
@@ -171,13 +181,12 @@ def tile_whnnaggregator_b_kernel(
                         transpose_keys(2)
                     elif (h, cb, i) != (0, 0, 0):
                         transpose_feat(2)
+                if (h, cb) == (0, 1):
+                    spread_degrees()
             source = [k_ps[i][:].rearrange("p (n b) -> p b n", b=GROUP) for i in range(2)]
             blocks = [keys[:, chunk(2 * h + i)].rearrange("p (b n) -> p b n", b=GROUP) for i in range(2)]
             nc.vector.tensor_scalar(blocks[0], source[0], k_scale[:], k_shift[:], ALU.mult, ALU.add)
             nc.scalar.activation(blocks[1], source[1], ACT.Identity, bias=k_shift[:], scale=k_scale[:])
-        deg_ps = psum_work.tile([LANES, BANK], F32, name="deg_ps", tag="work")
-        nc.tensor.matmul(deg_ps[:], ones_f[:], deg_row[:], start=True, stop=True)
-        nc.scalar.copy(deg[:, chunk(0)], deg_ps[:])
         norms(0)
         norms(1)
 
@@ -218,8 +227,8 @@ def tile_whnnaggregator_b_kernel(
             if nb == 5:
                 norms(2)
                 norms(3)
-            if nb in (2 * GROUP - 1, 3 * GROUP - 1):
-                for early in range(nb + 1 - 2 * GROUP, nb + 1 - GROUP):
+            if nb in (GROUP - 1, 2 * GROUP - 1):
+                for early in range(nb + 1 - GROUP, nb + 1):
                     prototypes(1, early)
         others = 0
         for nb in range(NB // 2, NB):

@@ -56,14 +56,12 @@ def tile_whnnaggregator_b_kernel(
         tc.psum_pool(name="psum_long", bufs=3) as psum_long,
         tc.psum_pool(name="psum_small", bufs=1) as psum_small,
     ):
-        ident_f = held.tile([LANES, LANES], F32, name="ident_f")
-        make_identity(nc, ident_f[:])
         ident_b = held.tile([LANES, LANES], BF16, name="ident_b")
-        nc.vector.tensor_copy(ident_b[:], ident_f[:])
+        make_identity(nc, ident_b[:])
+        deg_row = held.tile([LANES, BANK], F32, name="deg_row")
+        nc.vector.memset(deg_row[:], 0.0)
         ones_f = held.tile([LANES, LANES], F32, name="ones_f")
         nc.vector.memset(ones_f[:], 1.0)
-        deg_row = held.tile([LANES, BANK], F32, name="deg_row")
-        nc.gpsimd.memset(deg_row[:], 0.0)
         one_column = held.tile([LANES, 1], BF16, name="one_column")
         nc.vector.memset(one_column[:], 1.0)
 
@@ -245,6 +243,8 @@ def tile_whnnaggregator_b_kernel(
 
         sum_ps = psum_small.tile([LANES, QUARTERS], F32, name="sum_ps", tag="column")
         diagonal = held.tile([LANES, BANK], F32, name="diagonal")
+        ident_f = held.tile([LANES, LANES], F32, name="ident_f")
+        nc.vector.tensor_copy(ident_f[:], ident_b[:])
 
         def column_sum(q):
             for nb in range(NB):

@@ -1,7 +1,6 @@
 import math
 
 import concourse.mybir as mybir
-from concourse.masks import make_identity
 
 C, V, P, N, S = 512, 2048, 128, 1024, 2048
 TEMPERATURE = 0.1 + 1e-8
@@ -14,6 +13,7 @@ ACT = mybir.ActivationFunctionType
 AXIS = mybir.AxisListType
 
 LANES = 128
+SQUARE = 32
 BANK = 512
 CB = C // LANES
 NB = V // LANES
@@ -28,6 +28,10 @@ HALF = BANK // 2
 
 def block(i):
     return slice(i * LANES, (i + 1) * LANES)
+
+
+def square(i):
+    return slice(i * SQUARE, (i + 1) * SQUARE)
 
 
 def chunk(i):
@@ -56,12 +60,18 @@ def tile_whnnaggregator_b_kernel(
         tc.psum_pool(name="psum_long", bufs=3) as psum_long,
         tc.psum_pool(name="psum_small", bufs=1) as psum_small,
     ):
+        ones = held.tile([LANES, LANES], F32, name="ones")
+        nc.vector.memset(ones[:], 1.0)
+        count = held.tile([LANES, LANES], F32, name="count", align_bytes=64)
+        nc.vector.tensor_tensor_scan(count[:], ones[:], ones[:], 0.0, ALU.mult, ALU.add)
+        turned = held.tile([LANES, LANES], F32, name="turned", align_bytes=64)
+        nc.vector.transpose(turned[:], count[:])
+        same = held.tile([LANES, LANES], F32, name="same")
+        nc.vector.tensor_tensor(same[:], count[:], turned[:], ALU.is_equal)
         ident_b = held.tile([LANES, LANES], BF16, name="ident_b")
-        make_identity(nc, ident_b[:])
-        deg_row = held.tile([LANES, BANK], F32, name="deg_row")
-        nc.vector.memset(deg_row[:], 0.0)
-        ones_f = held.tile([LANES, LANES], F32, name="ones_f")
-        nc.vector.memset(ones_f[:], 1.0)
+        nc.vector.memset(ident_b[:], 0.0)
+        for a in range(LANES // SQUARE):
+            nc.vector.tensor_copy(ident_b[square(a), square(a)], same[square(a), square(a)])
         one_column = held.tile([LANES, 1], BF16, name="one_column")
         nc.vector.memset(one_column[:], 1.0)
 
@@ -84,7 +94,6 @@ def tile_whnnaggregator_b_kernel(
         load_feat(nc.scalar, 0, 0, chunk(0))
         load_feat(nc.sync, 0, 0, chunk(1))
         load_weights(nc.scalar, slice(1, CB))
-        nc.sync.dma_start(deg_row[0:1, :], inv_deg[0:1, chunk(0)])
         nc.scalar.dma_start(var[:], bn_var)
         for cb in range(1, CB):
             load_feat(nc.sync, 0, cb)
@@ -103,12 +112,13 @@ def tile_whnnaggregator_b_kernel(
         load_member(0, rows=slice(0, GROUP // 2))
         load_member(0, rows=slice(GROUP // 2, GROUP))
         load_member(1)
+        deg_rows = held.tile([LANES, SQUARE], F32, name="deg_rows", align_bytes=64)
+        for a in range(LANES // SQUARE):
+            nc.sync.dma_start(deg_rows[square(a), :], inv_deg.rearrange("o (b c) -> (o b) c", c=SQUARE))
         load_member(2)
         load_member(3, edges=chunk(0))
         load_member(3, edges=chunk(1))
-        deg = held.tile([LANES, N], F32, name="deg")
         nc.sync.dma_start(offsets[:], offs)
-        nc.sync.dma_start(deg[:, chunk(1)], inv_deg[0, chunk(1)].partition_broadcast(LANES))
         base_blocks = base.rearrange("(c cb) s -> cb c s", cb=CB)
         out_blocks = out.rearrange("(c cb) s -> cb c s", cb=CB)
         window = [held.tile([LANES, S], F32, name=f"window{cb}") for cb in range(CB)]
@@ -123,8 +133,16 @@ def tile_whnnaggregator_b_kernel(
         proto = held.tile([LANES, N], BF16, name="proto")
         soft = [held.tile([LANES, NB, BANK], BF16, name=f"soft{jc}") for jc in range(JC)]
         lane_sum = [held.tile([LANES, BANK], F32, name=f"lane_sum{i}") for i in range(2)]
-        lane_total = held.tile([LANES, BANK], F32, name="lane_total")
-        factor = [held.tile([LANES, BANK], F32, name=f"factor{jc}") for jc in range(JC)]
+        lane_total = held.tile([LANES, BANK], F32, name="lane_total", align_bytes=64)
+        lane_turned = held.tile([LANES, BANK], F32, name="lane_turned", align_bytes=64)
+        group_sum = [held.tile([LANES, BANK // SQUARE], F32, name=f"group_sum{jc}") for jc in range(JC)]
+        nc.vector.memset(group_sum[1][:], 0.0)
+        inverse = [held.tile([LANES, BANK // SQUARE], F32, name=f"inverse{jc}") for jc in range(JC)]
+        factor_repeated = [held.tile([LANES, BANK], F32, name=f"factor_repeated{jc}", align_bytes=64) for jc in range(JC)]
+        deg_columns = held.tile([LANES, SQUARE], F32, name="deg_columns", align_bytes=64)
+        deg_repeated = held.tile([LANES, N], F32, name="deg_repeated", align_bytes=64)
+        deg = held.tile([LANES, N], F32, name="deg", align_bytes=64)
+        factor = [held.tile([LANES, BANK], F32, name=f"factor{jc}", align_bytes=64) for jc in range(JC)]
 
 
         k_scale = held.tile([LANES, 1], F32, name="k_scale")
@@ -164,10 +182,11 @@ def tile_whnnaggregator_b_kernel(
             )
             nc.vector.tensor_reduce(neg_norm[:, group(g)], squares[:, group(g), :], axis=AXIS.X, op=ALU.add, negate=True)
 
-        def spread_degrees():
-            deg_ps = psum_work.tile([LANES, BANK], F32, name="deg_ps", tag="work")
-            nc.tensor.matmul(deg_ps[:], ones_f[:], deg_row[:], start=True, stop=True)
-            nc.scalar.copy(deg[:, chunk(0)], deg_ps[:])
+        def repeat(repeated, columns):
+            nc.scalar.copy(
+                repeated[:].rearrange("p (b r) -> p b r", r=SQUARE),
+                columns.unsqueeze(2).to_broadcast([LANES, columns.shape[1], SQUARE]),
+            )
 
         for h in range(HALVES):
             banks = [(psum_small, "spread"), (psum_small, "column")] if h == 0 else [(psum_work, "work")] * 2
@@ -179,14 +198,18 @@ def tile_whnnaggregator_b_kernel(
                         transpose_keys(2)
                     elif (h, cb, i) != (0, 0, 0):
                         transpose_feat(2)
-                if (h, cb) == (0, 1):
-                    spread_degrees()
             source = [k_ps[i][:].rearrange("p (n b) -> p b n", b=GROUP) for i in range(2)]
             blocks = [keys[:, chunk(2 * h + i)].rearrange("p (b n) -> p b n", b=GROUP) for i in range(2)]
             nc.vector.tensor_scalar(blocks[0], source[0], k_scale[:], k_shift[:], ALU.mult, ALU.add)
             nc.scalar.activation(blocks[1], source[1], ACT.Identity, bias=k_shift[:], scale=k_scale[:])
         norms(0)
         norms(1)
+
+        def first_sums():
+            nc.vector.transpose(lane_turned[:], lane_total[:])
+            nc.vector.tensor_reduce(
+                group_sum[0][:], lane_turned[:].rearrange("p (b c) -> p b c", c=SQUARE), axis=AXIS.X, op=ALU.add
+            )
 
         def weights_of(jc, nb):
             dot_ps = psum_work.tile([LANES, BANK], F32, name="dot_ps", tag="work")
@@ -201,6 +224,7 @@ def tile_whnnaggregator_b_kernel(
                 nc.vector.tensor_tensor(lane_sum[nb % 2][:], lane_sum[nb % 2][:], soft[0][:, nb, :], ALU.add)
             if (jc, nb) == (0, NB - 1):
                 nc.vector.tensor_tensor(lane_total[:], lane_sum[0][:], lane_sum[1][:], ALU.add)
+                first_sums()
 
         waiting_weights = [(jc, nb) for jc in range(JC) for nb in range(NB)]
 
@@ -222,6 +246,10 @@ def tile_whnnaggregator_b_kernel(
 
         for nb in range(NB):
             prototypes(0, nb)
+            if nb == 3:
+                nc.vector.transpose(deg_columns[:], deg_rows[:])
+                repeat(deg_repeated, deg_columns[:])
+                nc.vector.transpose(deg[:], deg_repeated[:])
             if nb == 5:
                 norms(2)
                 norms(3)
@@ -234,17 +262,14 @@ def tile_whnnaggregator_b_kernel(
             others += 1
             feed_scalar(others)
 
-
-        def first_factor():
-            total_ps = psum_small.tile([LANES, BANK], F32, name="total_ps", tag="spread")
-            nc.tensor.matmul(total_ps[:], ones_f[:], lane_total[:], start=True, stop=True)
-            nc.vector.reciprocal(factor[0][:], total_ps[:])
-            nc.vector.tensor_tensor(factor[0][:], factor[0][:], deg[:, chunk(0)], ALU.mult)
+        def factor_columns(jc):
+            total_ps = psum_small.tile([LANES, BANK // SQUARE], F32, name=f"total_ps{jc}", tag="spread")
+            nc.tensor.matmul(total_ps[:], same[:], group_sum[jc][:], start=True, stop=True)
+            nc.vector.reciprocal(inverse[jc][:], total_ps[:])
+            columns = slice(jc * (BANK // SQUARE), (jc + 1) * (BANK // SQUARE))
+            nc.vector.tensor_tensor(inverse[jc][:], inverse[jc][:], deg_columns[:, columns], ALU.mult)
 
         sum_ps = psum_small.tile([LANES, QUARTERS], F32, name="sum_ps", tag="column")
-        diagonal = held.tile([LANES, BANK], F32, name="diagonal")
-        ident_f = held.tile([LANES, LANES], F32, name="ident_f")
-        nc.vector.tensor_copy(ident_f[:], ident_b[:])
 
         def column_sum(q):
             for nb in range(NB):
@@ -252,15 +277,20 @@ def tile_whnnaggregator_b_kernel(
                     sum_ps[:, q : q + 1], soft[1][:, nb, block(q)], one_column[:], start=(nb == 0), stop=(nb == NB - 1)
                 )
             if q == QUARTERS - 1:
-                inv_sum = held.tile([LANES, QUARTERS], F32, name="inv_sum")
-                nc.vector.reciprocal(inv_sum[:], sum_ps[:])
-                for quarter in range(QUARTERS):
-                    nc.vector.tensor_scalar_mul(diagonal[:, block(quarter)], ident_f[:], inv_sum[:, quarter : quarter + 1])
+                for a in range(LANES // SQUARE):
+                    every_fourth = slice(a, BANK // SQUARE, LANES // SQUARE)
+                    nc.vector.tensor_copy(group_sum[1][square(a), every_fourth], sum_ps[square(a), :])
 
-        def second_factor():
-            spread_ps = psum_small.tile([LANES, BANK], F32, name="spread_ps", tag="spread")
-            nc.tensor.matmul(spread_ps[:], ones_f[:], diagonal[:], start=True, stop=True)
-            nc.vector.tensor_tensor(factor[1][:], spread_ps[:], deg[:, chunk(1)], ALU.mult)
+        to_place = []
+
+        def place():
+            for first, width, cb, agg in to_place:
+                piece = offsets[:, first // 16 : (first + width) // 16]
+                edges = slice(first % BANK, first % BANK + width)
+                nc.vector.tensor_tensor(window[cb][:].indirect(piece), agg[:], factor[first // BANK][:, edges], ALU.mult)
+                if first + width == N:
+                    nc.sync.dma_start(out_blocks[cb], window[cb][:])
+            to_place.clear()
 
         passes = [(0, BANK, (0, 1)), (0, BANK, (2,)), (0, BANK, (3,))]
         passes.extend((BANK + half * HALF, HALF, (cb,)) for cb in range(CB) for half in range(BANK // HALF))
@@ -275,16 +305,23 @@ def tile_whnnaggregator_b_kernel(
                     )
                     others += 1
                     feed_scalar(others)
-                if index == 0 and nb == NB - 3:
-                    first_factor()
+                if index == 0 and nb == NB - 1:
+                    factor_columns(0)
+                if index == 1 and nb == 2:
+                    repeat(factor_repeated[0], inverse[0][:])
+                    nc.vector.transpose(factor[0][:], factor_repeated[0][:])
+                    place()
                 if index == 2 and nb >= NB - QUARTERS:
                     column_sum(nb - (NB - QUARTERS))
-                if index == 3 and nb == NB - 1:
-                    second_factor()
+                if index == 3 and nb == NB // 2:
+                    factor_columns(1)
+                if index == 3 and nb == NB // 2 + 2:
+                    repeat(factor_repeated[1], inverse[1][:])
+                    place()
+                    nc.vector.transpose(factor[1][:], factor_repeated[1][:])
             for cb in together:
                 agg = held.tile([LANES, width], F32, name=f"agg{first}_{cb}")
                 nc.scalar.copy(agg[:], agg_ps[cb][:, 0:width])
-                piece = offsets[:, first // 16 : (first + width) // 16]
-                nc.vector.tensor_tensor(window[cb][:].indirect(piece), agg[:], factor[jc][:, edges], ALU.mult)
-                if first + width == N:
-                    nc.sync.dma_start(out_blocks[cb], window[cb][:])
+                to_place.append((first, width, cb, agg))
+            if index not in (0, 2):
+                place()

@@ -1,6 +1,7 @@
 import math
 
 import concourse.mybir as mybir
+from concourse.masks import make_identity
 
 C, V, P, N, S = 512, 2048, 128, 1024, 2048
 TEMPERATURE = 0.1 + 1e-8
@@ -60,6 +61,10 @@ def tile_whnnaggregator_b_kernel(
         tc.psum_pool(name="psum_long", bufs=3) as psum_long,
         tc.psum_pool(name="psum_small", bufs=1) as psum_small,
     ):
+        ident_b = held.tile([LANES, LANES], BF16, name="ident_b")
+        make_identity(nc, ident_b[:])
+        deg_row = held.tile([LANES, BANK], F32, name="deg_row")
+        nc.vector.memset(deg_row[:], 0.0)
         ones = held.tile([LANES, LANES], F32, name="ones")
         nc.vector.memset(ones[:], 1.0)
         count = held.tile([LANES, LANES], F32, name="count", align_bytes=64)
@@ -68,10 +73,6 @@ def tile_whnnaggregator_b_kernel(
         nc.vector.transpose(turned[:], count[:])
         same = held.tile([LANES, LANES], F32, name="same")
         nc.vector.tensor_tensor(same[:], count[:], turned[:], ALU.is_equal)
-        ident_b = held.tile([LANES, LANES], BF16, name="ident_b")
-        nc.vector.memset(ident_b[:], 0.0)
-        for a in range(LANES // SQUARE):
-            nc.vector.tensor_copy(ident_b[square(a), square(a)], same[square(a), square(a)])
         one_column = held.tile([LANES, 1], BF16, name="one_column")
         nc.vector.memset(one_column[:], 1.0)
 
@@ -94,6 +95,7 @@ def tile_whnnaggregator_b_kernel(
         load_feat(nc.scalar, 0, 0, chunk(0))
         load_feat(nc.sync, 0, 0, chunk(1))
         load_weights(nc.scalar, slice(1, CB))
+        nc.sync.dma_start(deg_row[0:1, :], inv_deg[0:1, chunk(0)])
         nc.scalar.dma_start(var[:], bn_var)
         for cb in range(1, CB):
             load_feat(nc.sync, 0, cb)
@@ -112,13 +114,15 @@ def tile_whnnaggregator_b_kernel(
         load_member(0, rows=slice(0, GROUP // 2))
         load_member(0, rows=slice(GROUP // 2, GROUP))
         load_member(1)
-        deg_rows = held.tile([LANES, SQUARE], F32, name="deg_rows", align_bytes=64)
-        for a in range(LANES // SQUARE):
-            nc.sync.dma_start(deg_rows[square(a), :], inv_deg.rearrange("o (b c) -> (o b) c", c=SQUARE))
         load_member(2)
         load_member(3, edges=chunk(0))
         load_member(3, edges=chunk(1))
+        deg = held.tile([LANES, N], F32, name="deg")
+        nc.sync.dma_start(deg[:, chunk(1)], inv_deg[0, chunk(1)].partition_broadcast(LANES))
         nc.sync.dma_start(offsets[:], offs)
+        deg_rows = held.tile([LANES, SQUARE], F32, name="deg_rows", align_bytes=64)
+        for a in range(LANES // SQUARE):
+            nc.sync.dma_start(deg_rows[square(a), :], inv_deg.rearrange("o (b c) -> (o b) c", c=SQUARE))
         base_blocks = base.rearrange("(c cb) s -> cb c s", cb=CB)
         out_blocks = out.rearrange("(c cb) s -> cb c s", cb=CB)
         window = [held.tile([LANES, S], F32, name=f"window{cb}") for cb in range(CB)]
@@ -140,8 +144,6 @@ def tile_whnnaggregator_b_kernel(
         inverse = [held.tile([LANES, BANK // SQUARE], F32, name=f"inverse{jc}") for jc in range(JC)]
         factor_repeated = [held.tile([LANES, BANK], F32, name=f"factor_repeated{jc}", align_bytes=64) for jc in range(JC)]
         deg_columns = held.tile([LANES, SQUARE], F32, name="deg_columns", align_bytes=64)
-        deg_repeated = held.tile([LANES, N], F32, name="deg_repeated", align_bytes=64)
-        deg = held.tile([LANES, N], F32, name="deg", align_bytes=64)
         factor = [held.tile([LANES, BANK], F32, name=f"factor{jc}", align_bytes=64) for jc in range(JC)]
 
 
@@ -182,11 +184,16 @@ def tile_whnnaggregator_b_kernel(
             )
             nc.vector.tensor_reduce(neg_norm[:, group(g)], squares[:, group(g), :], axis=AXIS.X, op=ALU.add, negate=True)
 
-        def repeat(repeated, columns):
-            nc.scalar.copy(
+        def repeat(copy, repeated, columns):
+            copy(
                 repeated[:].rearrange("p (b r) -> p b r", r=SQUARE),
                 columns.unsqueeze(2).to_broadcast([LANES, columns.shape[1], SQUARE]),
             )
+
+        def spread_degrees():
+            deg_ps = psum_work.tile([LANES, BANK], F32, name="deg_ps", tag="work")
+            nc.tensor.matmul(deg_ps[:], ones[:], deg_row[:], start=True, stop=True)
+            nc.scalar.copy(deg[:, chunk(0)], deg_ps[:])
 
         for h in range(HALVES):
             banks = [(psum_small, "spread"), (psum_small, "column")] if h == 0 else [(psum_work, "work")] * 2
@@ -198,6 +205,8 @@ def tile_whnnaggregator_b_kernel(
                         transpose_keys(2)
                     elif (h, cb, i) != (0, 0, 0):
                         transpose_feat(2)
+                if (h, cb) == (0, 1):
+                    spread_degrees()
             source = [k_ps[i][:].rearrange("p (n b) -> p b n", b=GROUP) for i in range(2)]
             blocks = [keys[:, chunk(2 * h + i)].rearrange("p (b n) -> p b n", b=GROUP) for i in range(2)]
             nc.vector.tensor_scalar(blocks[0], source[0], k_scale[:], k_shift[:], ALU.mult, ALU.add)
@@ -246,10 +255,6 @@ def tile_whnnaggregator_b_kernel(
 
         for nb in range(NB):
             prototypes(0, nb)
-            if nb == 3:
-                nc.vector.transpose(deg_columns[:], deg_rows[:])
-                repeat(deg_repeated, deg_columns[:])
-                nc.vector.transpose(deg[:], deg_repeated[:])
             if nb == 5:
                 norms(2)
                 norms(3)
@@ -261,6 +266,8 @@ def tile_whnnaggregator_b_kernel(
             prototypes(1, nb)
             others += 1
             feed_scalar(others)
+
+        nc.vector.transpose(deg_columns[:], deg_rows[:])
 
         def factor_columns(jc):
             total_ps = psum_small.tile([LANES, BANK // SQUARE], F32, name=f"total_ps{jc}", tag="spread")
@@ -307,21 +314,19 @@ def tile_whnnaggregator_b_kernel(
                     feed_scalar(others)
                 if index == 0 and nb == NB - 1:
                     factor_columns(0)
-                if index == 1 and nb == 2:
-                    repeat(factor_repeated[0], inverse[0][:])
+                    repeat(nc.vector.tensor_copy, factor_repeated[0], inverse[0][:])
                     nc.vector.transpose(factor[0][:], factor_repeated[0][:])
-                    place()
-                if index == 2 and nb >= NB - QUARTERS:
-                    column_sum(nb - (NB - QUARTERS))
-                if index == 3 and nb == NB // 2:
+                if index == 2 and QUARTERS <= nb < 2 * QUARTERS:
+                    column_sum(nb - QUARTERS)
+                if index == 2 and nb == NB - 1:
                     factor_columns(1)
-                if index == 3 and nb == NB // 2 + 2:
-                    repeat(factor_repeated[1], inverse[1][:])
+                if index == 3 and nb == 0:
+                    repeat(nc.scalar.copy, factor_repeated[1], inverse[1][:])
                     place()
                     nc.vector.transpose(factor[1][:], factor_repeated[1][:])
             for cb in together:
                 agg = held.tile([LANES, width], F32, name=f"agg{first}_{cb}")
                 nc.scalar.copy(agg[:], agg_ps[cb][:, 0:width])
                 to_place.append((first, width, cb, agg))
-            if index not in (0, 2):
+            if index != 2:
                 place()

@@ -80,10 +80,11 @@ def tile_whnnaggregator_b_kernel(
         weight_blocks = proj_w.rearrange("(c cb) p -> c cb p", cb=CB)
         feat = [held.tile([LANES, CB, V // HALVES], BF16, name=f"feat{h}") for h in range(HALVES)]
         feat_halves = vertex_feat.rearrange("(c cb) (h n) -> h c cb n", cb=CB, h=HALVES)
-        var = held.tile([LANES, 1], F32, name="var")
-        gamma = held.tile([LANES, 1], F32, name="gamma")
-        mean = held.tile([LANES, 1], F32, name="mean")
-        beta = held.tile([LANES, 1], F32, name="beta")
+        bn_rows = held.tile([LANES, SQUARE], F32, name="bn_rows", align_bytes=64)
+        nc.vector.memset(bn_rows[:], 0.0)
+
+        def load_bn(v, vector):
+            nc.scalar.dma_start(bn_rows[v:LANES:SQUARE, :], vector.rearrange("(a c) o -> a (o c)", c=SQUARE))
 
         def load_weights(queue, blocks):
             queue.dma_start(weights[:, blocks, :], weight_blocks[:, blocks, :])
@@ -96,13 +97,13 @@ def tile_whnnaggregator_b_kernel(
         load_feat(nc.sync, 0, 0, chunk(1))
         load_weights(nc.scalar, slice(1, CB))
         nc.sync.dma_start(deg_row[0:1, :], inv_deg[0:1, chunk(0)])
-        nc.scalar.dma_start(var[:], bn_var)
+        load_bn(0, bn_var)
         for cb in range(1, CB):
             load_feat(nc.sync, 0, cb)
         load_feat(nc.sync, 1, 0)
-        nc.scalar.dma_start(gamma[:], bn_gamma)
-        nc.scalar.dma_start(mean[:], bn_mean)
-        nc.scalar.dma_start(beta[:], bn_beta)
+        load_bn(1, bn_gamma)
+        load_bn(2, bn_mean)
+        load_bn(3, bn_beta)
         for cb in range(1, CB):
             load_feat(nc.sync, 1, cb)
         member = held.tile([LANES, NB, N], BF16, name="member")
@@ -149,10 +150,13 @@ def tile_whnnaggregator_b_kernel(
 
         k_scale = held.tile([LANES, 1], F32, name="k_scale")
         k_shift = held.tile([LANES, 1], F32, name="k_shift")
-        nc.scalar.activation(k_scale[:], var[:], ACT.Abs_reciprocal_sqrt, bias=BN_EPS)
-        nc.vector.tensor_mul(k_scale[:], k_scale[:], gamma[:])
-        nc.vector.tensor_mul(k_shift[:], mean[:], k_scale[:])
-        nc.vector.tensor_sub(k_shift[:], beta[:], k_shift[:])
+        bn_columns = held.tile([LANES, SQUARE], F32, name="bn_columns", align_bytes=64)
+        nc.vector.transpose(bn_columns[:], bn_rows[:])
+        var, gamma, mean, beta = (bn_columns[:, v : v + 1] for v in range(4))
+        nc.scalar.activation(k_scale[:], var, ACT.Abs_reciprocal_sqrt, bias=BN_EPS)
+        nc.vector.tensor_mul(k_scale[:], k_scale[:], gamma)
+        nc.vector.tensor_mul(k_shift[:], mean, k_scale[:])
+        nc.vector.tensor_sub(k_shift[:], beta, k_shift[:])
 
         feat_blocks = [(h, cb, i) for h in range(HALVES) for cb in range(CB) for i in range(OCTET)]
         key_blocks = [(g, i) for g in range(NB // GROUP) for i in range(GROUP)]
@@ -193,7 +197,7 @@ def tile_whnnaggregator_b_kernel(
         def spread_degrees():
             deg_ps = psum_work.tile([LANES, BANK], F32, name="deg_ps", tag="work")
             nc.tensor.matmul(deg_ps[:], ones[:], deg_row[:], start=True, stop=True)
-            nc.scalar.copy(deg[:, chunk(0)], deg_ps[:])
+            return deg_ps
 
         for h in range(HALVES):
             banks = [(psum_small, "spread"), (psum_small, "column")] if h == 0 else [(psum_work, "work")] * 2
@@ -206,11 +210,12 @@ def tile_whnnaggregator_b_kernel(
                     elif (h, cb, i) != (0, 0, 0):
                         transpose_feat(2)
                 if (h, cb) == (0, 1):
-                    spread_degrees()
+                    deg_ps = spread_degrees()
             source = [k_ps[i][:].rearrange("p (n b) -> p b n", b=GROUP) for i in range(2)]
             blocks = [keys[:, chunk(2 * h + i)].rearrange("p (b n) -> p b n", b=GROUP) for i in range(2)]
             nc.vector.tensor_scalar(blocks[0], source[0], k_scale[:], k_shift[:], ALU.mult, ALU.add)
             nc.scalar.activation(blocks[1], source[1], ACT.Identity, bias=k_shift[:], scale=k_scale[:])
+        nc.vector.tensor_copy(deg[:, chunk(0)], deg_ps[:])
         norms(0)
         norms(1)
 

import math

import concourse.mybir as mybir
from concourse.masks import make_identity

C, V, P, N, S = 512, 2048, 128, 1024, 2048
TEMPERATURE = 0.1 + 1e-8
BN_EPS = 1e-5
FLOPS = 2 * (C * P * V + 2 * P * V * N + C * V * N)

BF16, F32, U16 = mybir.dt.bfloat16, mybir.dt.float32, mybir.dt.uint16
ALU = mybir.AluOpType
ACT = mybir.ActivationFunctionType
AXIS = mybir.AxisListType

LANES = 128
SQUARE = 32
BANK = 512
CB = C // LANES
NB = V // LANES
JC = N // BANK
QUARTERS = BANK // LANES
GROUP = 4
OCTET = 8
HALVES = NB // OCTET
LEAD = 4
HALF = BANK // 2


def block(i):
    return slice(i * LANES, (i + 1) * LANES)


def square(i):
    return slice(i * SQUARE, (i + 1) * SQUARE)


def chunk(i):
    return slice(i * BANK, (i + 1) * BANK)


def vertices(i):
    return slice(i // GROUP * BANK + i % GROUP, (i // GROUP + 1) * BANK, GROUP)


def group(i):
    return slice(i * GROUP, (i + 1) * GROUP)


def octet(i):
    return slice(i * OCTET, (i + 1) * OCTET)


def tile_whnnaggregator_b_kernel(
    tc, vertex_feat, incidence, inv_deg, proj_w, bn_gamma, bn_beta, bn_mean, bn_var, base, offs, out
):
    nc = tc.nc
    with (
        tc.tile_pool(name="held", bufs=1) as held,
        tc.psum_pool(name="psum_work", bufs=3) as psum_work,
        tc.psum_pool(name="psum_long", bufs=3) as psum_long,
        tc.psum_pool(name="psum_small", bufs=1) as psum_small,
    ):
        ident_b = held.tile([LANES, LANES], BF16, name="ident_b")
        make_identity(nc, ident_b[:])
        deg_row = held.tile([LANES, BANK], F32, name="deg_row")
        nc.vector.memset(deg_row[:], 0.0)
        ones = held.tile([LANES, LANES], F32, name="ones")
        nc.vector.memset(ones[:], 1.0)
        count = held.tile([LANES, LANES], F32, name="count", align_bytes=64)
        nc.vector.tensor_tensor_scan(count[:], ones[:], ones[:], 0.0, ALU.mult, ALU.add)
        turned = held.tile([LANES, LANES], F32, name="turned", align_bytes=64)
        nc.vector.transpose(turned[:], count[:])
        same = held.tile([LANES, LANES], F32, name="same")
        nc.vector.tensor_tensor(same[:], count[:], turned[:], ALU.is_equal)
        one_column = held.tile([LANES, 1], BF16, name="one_column")
        nc.vector.memset(one_column[:], 1.0)

        weights = held.tile([LANES, CB, P], BF16, name="weights")
        weight_blocks = proj_w.rearrange("(c cb) p -> c cb p", cb=CB)
        feat = [held.tile([LANES, CB, V // HALVES], BF16, name=f"feat{h}") for h in range(HALVES)]
        feat_halves = vertex_feat.rearrange("(c cb) (h n) -> h c cb n", cb=CB, h=HALVES)
        bn_rows = held.tile([LANES, SQUARE], F32, name="bn_rows", align_bytes=64)
        nc.vector.memset(bn_rows[:], 0.0)

        def load_bn(v, vector):
            nc.scalar.dma_start(bn_rows[v:LANES:SQUARE, :], vector.rearrange("(a c) o -> a (o c)", c=SQUARE))

        def load_weights(queue, blocks):
            queue.dma_start(weights[:, blocks, :], weight_blocks[:, blocks, :])

        def load_feat(queue, h, cb, columns=slice(0, V // HALVES)):
            queue.dma_start(feat[h][:, cb, columns], feat_halves[h][:, cb, columns])

        load_weights(nc.sync, slice(0, 1))
        load_feat(nc.scalar, 0, 0, chunk(0))
        load_feat(nc.sync, 0, 0, chunk(1))
        load_weights(nc.scalar, slice(1, CB))
        nc.sync.dma_start(deg_row[0:1, :], inv_deg[0:1, chunk(0)])
        load_bn(0, bn_var)
        for cb in range(1, CB):
            load_feat(nc.sync, 0, cb)
        load_feat(nc.sync, 1, 0)
        load_bn(1, bn_gamma)
        load_bn(2, bn_mean)
        load_bn(3, bn_beta)
        for cb in range(1, CB):
            load_feat(nc.sync, 1, cb)
        member = held.tile([LANES, NB, N], BF16, name="member")
        incidence_groups = incidence.rearrange("(a n b) j -> a n b j", n=LANES, b=GROUP)
        offsets = held.tile([LANES, N // 16], U16, name="offsets")
        def load_member(a, rows=slice(0, GROUP), edges=slice(0, N)):
            nc.sync.dma_start(member[:, group(a), :][:, rows, edges], incidence_groups[a][:, rows, edges])

        load_member(0, rows=slice(0, GROUP // 2))
        load_member(0, rows=slice(GROUP // 2, GROUP))
        load_member(1)
        load_member(2)
        load_member(3, edges=chunk(0))
        load_member(3, edges=chunk(1))
        deg = held.tile([LANES, N], F32, name="deg")
        nc.sync.dma_start(deg[:, chunk(1)], inv_deg[0, chunk(1)].partition_broadcast(LANES))
        nc.sync.dma_start(offsets[:], offs)
        deg_rows = held.tile([LANES, SQUARE], F32, name="deg_rows", align_bytes=64)
        for a in range(LANES // SQUARE):
            nc.sync.dma_start(deg_rows[square(a), :], inv_deg.rearrange("o (b c) -> (o b) c", c=SQUARE))
        base_blocks = base.rearrange("(c cb) s -> cb c s", cb=CB)
        out_blocks = out.rearrange("(c cb) s -> cb c s", cb=CB)
        window = [held.tile([LANES, S], F32, name=f"window{cb}") for cb in range(CB)]
        for cb in range(CB):
            nc.sync.dma_start(window[cb][:], base_blocks[cb])

        keys = held.tile([LANES, V], BF16, name="keys")
        keys_t = held.tile([LANES, NB, P], BF16, name="keys_t")
        squares = held.tile([LANES, NB, P], F32, name="squares")
        neg_norm = held.tile([LANES, NB], F32, name="neg_norm")
        feat_t = held.tile([LANES, CB, NB, LANES], BF16, name="feat_t")
        proto = held.tile([LANES, N], BF16, name="proto")
        soft = [held.tile([LANES, NB, BANK], BF16, name=f"soft{jc}") for jc in range(JC)]
        lane_sum = [held.tile([LANES, BANK], F32, name=f"lane_sum{i}") for i in range(2)]
        lane_total = held.tile([LANES, BANK], F32, name="lane_total", align_bytes=64)
        lane_turned = held.tile([LANES, BANK], F32, name="lane_turned", align_bytes=64)
        group_sum = [held.tile([LANES, BANK // SQUARE], F32, name=f"group_sum{jc}") for jc in range(JC)]
        nc.vector.memset(group_sum[1][:], 0.0)
        inverse = [held.tile([LANES, BANK // SQUARE], F32, name=f"inverse{jc}") for jc in range(JC)]
        factor_repeated = [held.tile([LANES, BANK], F32, name=f"factor_repeated{jc}", align_bytes=64) for jc in range(JC)]
        deg_columns = held.tile([LANES, SQUARE], F32, name="deg_columns", align_bytes=64)
        factor = [held.tile([LANES, BANK], F32, name=f"factor{jc}", align_bytes=64) for jc in range(JC)]


        k_scale = held.tile([LANES, 1], F32, name="k_scale")
        k_shift = held.tile([LANES, 1], F32, name="k_shift")
        bn_columns = held.tile([LANES, SQUARE], F32, name="bn_columns", align_bytes=64)
        nc.vector.transpose(bn_columns[:], bn_rows[:])
        var, gamma, mean, beta = (bn_columns[:, v : v + 1] for v in range(4))
        nc.scalar.activation(k_scale[:], var, ACT.Abs_reciprocal_sqrt, bias=BN_EPS)
        nc.vector.tensor_mul(k_scale[:], k_scale[:], gamma)
        nc.vector.tensor_mul(k_shift[:], mean, k_scale[:])
        nc.vector.tensor_sub(k_shift[:], beta, k_shift[:])

        feat_blocks = [(h, cb, i) for h in range(HALVES) for cb in range(CB) for i in range(OCTET)]
        key_blocks = [(g, i) for g in range(NB // GROUP) for i in range(GROUP)]
        ft_ps, kt_ps = {}, {}

        def transpose_feat(count):
            for h, cb, i in feat_blocks[:count]:
                if i == 0:
                    pool, tag = (psum_small, "spread") if (h, cb) == (HALVES - 1, CB - 2) else (psum_long, "long")
                    ft_ps[h, cb] = pool.tile([LANES, OCTET, LANES], BF16, name=f"ft_ps{h}_{cb}", tag=tag)
                nc.tensor.transpose(ft_ps[h, cb][:, i, :], feat[h][:, cb, vertices(i)], ident_b[:])
                if i == OCTET - 1:
                    nc.vector.tensor_copy(feat_t[:, cb, octet(h), :], ft_ps[h, cb][:])
            feat_blocks[:count] = []

        def transpose_keys(count):
            for g, i in key_blocks[:count]:
                if i == 0:
                    pool, tag = (psum_work, "work") if g > 1 else (psum_small, ("spread", "column")[g])
                    kt_ps[g] = pool.tile([LANES, GROUP, P], BF16, name=f"kt_ps{g}", tag=tag)
                nc.tensor.transpose(kt_ps[g][:, i, :], keys[:, block(g * GROUP + i)], ident_b[:])
                if i == GROUP - 1:
                    nc.scalar.copy(keys_t[:, group(g), :], kt_ps[g][:])
            key_blocks[:count] = []

        def norms(g):
            nc.scalar.activation(
                squares[:, group(g), :], keys_t[:, group(g), :], ACT.Square, scale=math.sqrt(1.0 / TEMPERATURE)
            )
            nc.vector.tensor_reduce(neg_norm[:, group(g)], squares[:, group(g), :], axis=AXIS.X, op=ALU.add, negate=True)

        def repeat(copy, repeated, columns):
            copy(
                repeated[:].rearrange("p (b r) -> p b r", r=SQUARE),
                columns.unsqueeze(2).to_broadcast([LANES, columns.shape[1], SQUARE]),
            )

        def spread_degrees():
            deg_ps = psum_work.tile([LANES, BANK], F32, name="deg_ps", tag="work")
            nc.tensor.matmul(deg_ps[:], ones[:], deg_row[:], start=True, stop=True)
            return deg_ps

        for h in range(HALVES):
            banks = [(psum_small, "spread"), (psum_small, "column")] if h == 0 else [(psum_work, "work")] * 2
            k_ps = [pool.tile([LANES, BANK], F32, name=f"k_ps{h}_{i}", tag=tag) for i, (pool, tag) in enumerate(banks)]
            for cb in range(CB):
                for i in range(2):
                    nc.tensor.matmul(k_ps[i][:], weights[:, cb, :], feat[h][:, cb, chunk(i)], start=(cb == 0), stop=(cb == CB - 1))
                    if h == 1 and 3 <= 2 * cb + i < 7:
                        transpose_keys(2)
                    elif (h, cb, i) != (0, 0, 0):
                        transpose_feat(2)
                if (h, cb) == (0, 1):
                    deg_ps = spread_degrees()
            source = [k_ps[i][:].rearrange("p (n b) -> p b n", b=GROUP) for i in range(2)]
            blocks = [keys[:, chunk(2 * h + i)].rearrange("p (b n) -> p b n", b=GROUP) for i in range(2)]
            nc.vector.tensor_scalar(blocks[0], source[0], k_scale[:], k_shift[:], ALU.mult, ALU.add)
            nc.scalar.activation(blocks[1], source[1], ACT.Identity, bias=k_shift[:], scale=k_scale[:])
        nc.vector.tensor_copy(deg[:, chunk(0)], deg_ps[:])
        norms(0)
        norms(1)

        def first_sums():
            nc.vector.transpose(lane_turned[:], lane_total[:])
            nc.vector.tensor_reduce(
                group_sum[0][:], lane_turned[:].rearrange("p (b c) -> p b c", c=SQUARE), axis=AXIS.X, op=ALU.add
            )

        def weights_of(jc, nb):
            dot_ps = psum_work.tile([LANES, BANK], F32, name="dot_ps", tag="work")
            nc.tensor.matmul(dot_ps[:], keys[:, block(nb)], proto[:, chunk(jc)], start=True, stop=True)
            transpose_feat(1)
            nc.scalar.activation(
                soft[jc][:, nb, :], dot_ps[:], ACT.Exp, bias=neg_norm[:, nb : nb + 1], scale=2.0 / TEMPERATURE
            )
            if jc == 0 and nb in (2, 3):
                nc.vector.tensor_tensor(lane_sum[nb % 2][:], soft[0][:, nb - 2, :], soft[0][:, nb, :], ALU.add)
            if jc == 0 and nb > 3:
                nc.vector.tensor_tensor(lane_sum[nb % 2][:], lane_sum[nb % 2][:], soft[0][:, nb, :], ALU.add)
            if (jc, nb) == (0, NB - 1):
                nc.vector.tensor_tensor(lane_total[:], lane_sum[0][:], lane_sum[1][:], ALU.add)
                first_sums()

        waiting_weights = [(jc, nb) for jc in range(JC) for nb in range(NB)]

        def feed_scalar(others):
            due = (others - LEAD) * 3 // 5 + 1
            while waiting_weights and JC * NB - len(waiting_weights) < due:
                weights_of(*waiting_weights.pop(0))

        proto_ps = [psum_small.tile([LANES, BANK], F32, name=f"proto_ps{jc}", tag=tag) for jc, tag in enumerate(("spread", "column"))]

        def prototypes(jc, nb):
            nc.tensor.matmul(proto_ps[jc][:], keys_t[:, nb, :], member[:, nb, chunk(jc)], start=(nb == 0), stop=(nb == NB - 1))
            if jc == 0 and 2 <= nb < 6:
                transpose_keys(2)
            else:
                transpose_feat(1)
            if nb == NB - 1:
                nc.vector.tensor_tensor(proto[:, chunk(jc)], proto_ps[jc][:], deg[:, chunk(jc)], ALU.mult)

        for nb in range(NB):
            prototypes(0, nb)
            if nb == 5:
                norms(2)
                norms(3)
            if nb in (GROUP - 1, 2 * GROUP - 1):
                for early in range(nb + 1 - GROUP, nb + 1):
                    prototypes(1, early)
        others = 0
        for nb in range(NB // 2, NB):
            prototypes(1, nb)
            others += 1
            feed_scalar(others)

        nc.vector.transpose(deg_columns[:], deg_rows[:])

        def factor_columns(jc):
            total_ps = psum_small.tile([LANES, BANK // SQUARE], F32, name=f"total_ps{jc}", tag="spread")
            nc.tensor.matmul(total_ps[:], same[:], group_sum[jc][:], start=True, stop=True)
            nc.vector.reciprocal(inverse[jc][:], total_ps[:])
            columns = slice(jc * (BANK // SQUARE), (jc + 1) * (BANK // SQUARE))
            nc.vector.tensor_tensor(inverse[jc][:], inverse[jc][:], deg_columns[:, columns], ALU.mult)

        sum_ps = psum_small.tile([LANES, QUARTERS], F32, name="sum_ps", tag="column")

        def column_sum(q):
            for nb in range(NB):
                nc.tensor.matmul(
                    sum_ps[:, q : q + 1], soft[1][:, nb, block(q)], one_column[:], start=(nb == 0), stop=(nb == NB - 1)
                )
            if q == QUARTERS - 1:
                for a in range(LANES // SQUARE):
                    every_fourth = slice(a, BANK // SQUARE, LANES // SQUARE)
                    nc.vector.tensor_copy(group_sum[1][square(a), every_fourth], sum_ps[square(a), :])

        to_place = []

        def place():
            for first, width, cb, agg in to_place:
                piece = offsets[:, first // 16 : (first + width) // 16]
                edges = slice(first % BANK, first % BANK + width)
                nc.vector.tensor_tensor(window[cb][:].indirect(piece), agg[:], factor[first // BANK][:, edges], ALU.mult)
                if first + width == N:
                    nc.sync.dma_start(out_blocks[cb], window[cb][:])
            to_place.clear()

        passes = [(0, BANK, (0, 1)), (0, BANK, (2,)), (0, BANK, (3,))]
        passes.extend((BANK + half * HALF, HALF, (cb,)) for cb in range(CB) for half in range(BANK // HALF))
        for index, (first, width, together) in enumerate(passes):
            jc = first // BANK
            edges = slice(first % BANK, first % BANK + width)
            agg_ps = {cb: psum_long.tile([LANES, BANK], F32, name=f"agg_ps{cb}", tag="long") for cb in together}
            for nb in range(NB):
                for cb in together:
                    nc.tensor.matmul(
                        agg_ps[cb][:, 0:width], feat_t[:, cb, nb, :], soft[jc][:, nb, edges], start=(nb == 0), stop=(nb == NB - 1)
                    )
                    others += 1
                    feed_scalar(others)
                if index == 0 and nb == NB - 1:
                    factor_columns(0)
                    repeat(nc.vector.tensor_copy, factor_repeated[0], inverse[0][:])
                    nc.vector.transpose(factor[0][:], factor_repeated[0][:])
                if index == 2 and QUARTERS <= nb < 2 * QUARTERS:
                    column_sum(nb - QUARTERS)
                if index == 2 and nb == NB - 1:
                    factor_columns(1)
                if index == 3 and nb == 0:
                    repeat(nc.scalar.copy, factor_repeated[1], inverse[1][:])
                    place()
                    nc.vector.transpose(factor[1][:], factor_repeated[1][:])
            for cb in together:
                agg = held.tile([LANES, width], F32, name=f"agg{first}_{cb}")
                nc.scalar.copy(agg[:], agg_ps[cb][:, 0:width])
                to_place.append((first, width, cb, agg))
            if index != 2:
                place()
